import numpy as np
import ml_dtypes


def mxq(x, axis, fmt="e4m3"):
    dtype, down = {"e4m3": (ml_dtypes.float8_e4m3fn, 7), "e5m2": (ml_dtypes.float8_e5m2, 14)}[fmt]
    v = np.moveaxis(np.asarray(x, np.float32).astype(ml_dtypes.bfloat16).astype(np.float64), axis, -1)
    blocks = v.reshape(v.shape[:-1] + (-1, 32))
    amax = np.abs(blocks).max(-1, keepdims=True)
    byte = np.maximum(np.where(amax > 0, np.frexp(amax)[1] - 1 + 127, 0) - down, 1)
    scale = np.exp2(byte - 127.0)
    codes = (blocks / scale).astype(np.float32).astype(dtype).astype(np.float64)
    return np.moveaxis((codes * scale).reshape(v.shape), -1, axis)


WIDE = False


def mx_kscale(k):
    if not WIDE:
        return np.ones(k)
    levels = np.array([10, -10, 5, -5, 0])
    a = np.random.permutation(np.resize(levels, k // 512 * 4)).reshape(k // 512, 4)
    idx = np.arange(k)
    return np.exp2(a[idx // 512, idx % 128 // 32])


BF16 = ml_dtypes.bfloat16


def bf(x):
    return np.asarray(x, np.float32).astype(BF16)


def f64(x):
    return np.asarray(x).astype(np.float64)


B, N, D, F, M1, M2 = 4, 512, 512, 512, 3, 5
EPS = 1e-12


def erf(z):
    a = np.clip(z, -6.0, 6.0)
    a2 = 2.0 * a * a
    term = a.copy()
    tot = a.copy()
    for k in range(1, 120):
        term = term * (a2 / (2 * k + 1))
        tot = tot + term
    return 2.0 / np.sqrt(np.pi) * np.exp(-a * a) * tot


def gelu(v):
    return 0.5 * v * (1.0 + erf(v / np.sqrt(2.0)))


def setup_inputs():
    s = mx_kscale(D)
    return {'x': bf(np.random.standard_normal((B, N, D, M1)) * s[:, None]),
            'w_in': bf(np.random.standard_normal((D, F)) / np.sqrt(D) / s[:, None]),
            'scale': bf(1.0 + 0.1 * np.random.standard_normal((1, 1, F))),
            'bias': bf(0.3 * np.random.standard_normal((1, 1, F))),
            'w_out': bf(np.random.standard_normal((F, D)) / np.sqrt(F))}


def reference(x, w_in, scale, bias, w_out):
    xq = mxq(f64(x), 2, 'e4m3')
    h = np.swapaxes(np.swapaxes(xq, -1, -2) @ mxq(f64(w_in), 0, 'e4m3'), -1, -2)
    norm = np.maximum(np.sqrt(np.sum(h * h, axis=-1, keepdims=True)), EPS)
    phase = h / norm
    gated = gelu(norm[..., 0] * f64(scale) + f64(bias))[..., None]
    g = gated * phase
    y = np.swapaxes(mxq(g, 2, 'e4m3'), -1, -2) @ mxq(f64(w_out), 0, 'e4m3')
    return np.swapaxes(y, -1, -2)

@@ -1,0 +1,299 @@
+from contextlib import ExitStack
+
+import concourse.mybir as mybir
+from concourse.masks import make_identity
+
+FLOPS = 2 * 2 * 2048 * 3 * 512 * 512
+
+BF16 = mybir.dt.bfloat16
+F32 = mybir.dt.float32
+U32 = mybir.dt.uint32
+U8 = mybir.dt.uint8
+FP8X4 = mybir.dt.float8_e4m3fn_x4
+ACT = mybir.ActivationFunctionType
+ALU = mybir.AluOpType
+
+P = 128
+NCH = 16
+E = 1536
+TOK = 2048
+GROUPS = ((0,), (1,), (2, 3), (4, 5), (6, 7))
+S_COPIES = ((0, 1), (1, 1), (3, 1), (5, 1))
+V_ADDS = ()
+XS_BUFS = 6
+RN_MAX = 1.0e12
+
+
+def tile_feedforwardse3_pa_t_kernel(tc, x, w_in, scale, bias, w_out, out):
+    nc = tc.nc
+    xv = x.rearrange("b n d m -> (b n) (d m)").rearrange("(p c) e -> p c e", c=NCH)
+    ov = out.rearrange("b n d m -> (b n) (d m)").rearrange("(p c) e -> p c e", c=NCH)
+
+    with ExitStack() as ctx:
+        ctx.enter_context(tc.manual_schedule())
+        keep = ctx.enter_context(tc.tile_pool(name="keep", bufs=1))
+
+        ident = keep.tile([P, P], BF16, name="ident")
+        wq_in = keep.tile([P, 512], U32, name="wq_in", align_bytes=64)
+        ws_in = keep.tile([P, 512], U8, name="ws_in", align_bytes=64)
+        wq_out = keep.tile([P, 512], U32, name="wq_out", align_bytes=64)
+        ws_out = keep.tile([P, 512], U8, name="ws_out", align_bytes=64)
+        xq = keep.tile([P, 3, TOK], U32, name="xq", align_bytes=64)
+        xsc = keep.tile([P, 3, TOK], U8, name="xsc", align_bytes=64)
+        a1 = keep.tile([P, 4, TOK], F32, name="a1")
+        a2 = keep.tile([P, 4, TOK], F32, name="a2")
+        sc_raw = keep.tile([P, 4], BF16, name="sc_raw")
+        bi_raw = keep.tile([P, 4], BF16, name="bi_raw")
+        sc = keep.tile([P, 4], F32, name="sc")
+        bi = keep.tile([P, 4], F32, name="bi")
+        one = keep.tile([P, 1], F32, name="one")
+        one2 = keep.tile([P, 1], F32, name="one2")
+
+        def span(gi):
+            pairs = GROUPS[gi]
+            return 256 * pairs[0], 256 * len(pairs)
+
+        def quantise(codes, scales, src):
+            nc.vector.quantize_mx(out=codes.bitcast(FP8X4), scales=scales, in_=src)
+
+        def mx(dst, lw, ls, rw, rs):
+            nc.tensor.matmul_mx(
+                out=dst,
+                lhsT=lw.bitcast(FP8X4),
+                lhsT_scale=ls,
+                rhs=rw.bitcast(FP8X4),
+                rhs_scale=rs,
+                start=True,
+                stop=True,
+            )
+
+        with ExitStack() as actx:
+            xpool = actx.enter_context(tc.tile_pool(name="xpool", bufs=XS_BUFS))
+            gpool = actx.enter_context(tc.tile_pool(name="gpool", bufs=6))
+            qpool = actx.enter_context(tc.tile_pool(name="qpool", bufs=3))
+            spool = actx.enter_context(tc.tile_pool(name="spool", bufs=2))
+            wpool = actx.enter_context(tc.tile_pool(name="wpool", bufs=1))
+            ps_t = actx.enter_context(tc.psum_pool(name="ps_t", bufs=3))
+            ps_h = actx.enter_context(tc.psum_pool(name="ps_h", bufs=5))
+
+            xs = {}
+            xg = {}
+
+            def load_pair(q):
+                xs[q] = xpool.tile([P, 2, E], BF16, name="xs", tag="xs")
+                nc.sync.dma_start(out=xs[q][:], in_=xv[:, 2 * q : 2 * q + 2, :])
+
+            def transposes(q, m):
+                pt = ps_t.tile([P, 2, 4, P], BF16, name="pt", tag="pt")
+                for u in range(2):
+                    src = xs[q][:, u, :].rearrange("p (d m) -> p d m", m=3)
+                    for j in range(4):
+                        nc.tensor.transpose(pt[:, u, j, :], src[:, P * j : P * (j + 1), m], ident[:])
+                return pt
+
+            def copy_out(gi, q, m, pt):
+                if (gi, m) not in xg:
+                    xg[(gi, m)] = gpool.tile([P, 512, 4], BF16, name="xg", tag="xg", align_bytes=64)
+                h = q - GROUPS[gi][0]
+                dst = xg[(gi, m)][:, 256 * h : 256 * (h + 1), :].rearrange("p (c t) j -> p c t j", c=2)
+                src = pt[:].rearrange("p c j t -> p c t j")
+                if (q, m) in S_COPIES:
+                    nc.scalar.copy(out=dst, in_=src)
+                else:
+                    nc.vector.tensor_copy(out=dst, in_=src)
+
+            def quantise_x(gi):
+                t0, w = span(gi)
+                for m in range(3):
+                    quantise(
+                        xq[:, m, t0 : t0 + w],
+                        xsc[:, m, t0 : t0 + w],
+                        xg[(gi, m)][:, :w, :].rearrange("p c j -> p (c j)"),
+                    )
+
+            def rsqrt(gi, j0, j1):
+                t0, w = span(gi)
+                nc.scalar.activation(
+                    out=a2[:, j0:j1, t0 : t0 + w], in_=a1[:, j0:j1, t0 : t0 + w], func=ACT.Abs_reciprocal_sqrt
+                )
+
+            def norm(gi, j0, j1):
+                t0, w = span(gi)
+                nc.vector.scalar_tensor_tensor(
+                    out=a1[:, j0:j1, t0 : t0 + w],
+                    in0=a2[:, j0:j1, t0 : t0 + w],
+                    scalar=RN_MAX,
+                    in1=a1[:, j0:j1, t0 : t0 + w],
+                    op0=ALU.min,
+                    op1=ALU.mult,
+                )
+
+            wr_in = wpool.tile([P, 4, 512], BF16, name="wr_in")
+            wg_in = wpool.tile([P, 512, 4], BF16, name="wg_in", align_bytes=64)
+            wr_out = wpool.tile([P, 4, 512], BF16, name="wr_out")
+            wg_out = wpool.tile([P, 512, 4], BF16, name="wg_out", align_bytes=64)
+            nc.scalar.dma_start(out=wr_in[:], in_=w_in.rearrange("(j p) f -> p j f", p=P))
+            load_pair(0)
+            nc.scalar.dma_start(out=sc_raw[:], in_=scale.rearrange("a b (p j) -> (a b p) j", j=4))
+            nc.scalar.dma_start(out=bi_raw[:], in_=bias.rearrange("a b (p j) -> (a b p) j", j=4))
+            make_identity(nc, ident[:])
+            nc.vector.memset(one[:], 1.0)
+            nc.scalar.activation(out=one2[:], in_=one[:], func=ACT.Abs_reciprocal_sqrt)
+            for q in range(1, XS_BUFS):
+                load_pair(q)
+            nc.sync.dma_start(out=wr_out[:], in_=w_out.rearrange("(p j) d -> p j d", j=4))
+
+            wsrc = wr_in[:].rearrange("p j (b a) -> p a b j", a=4)
+            wdst = wg_in[:].rearrange("p (a b) j -> p a b j", a=4)
+            nc.vector.tensor_copy(out=wdst[:, 0:2, :, :], in_=wsrc[:, 0:2, :, :])
+            nc.scalar.copy(out=wdst[:, 2:4, :, :], in_=wsrc[:, 2:4, :, :])
+
+            first = [(q, m) for q in GROUPS[0] for m in range(3)]
+            pts = [transposes(q, m) for (q, m) in first]
+            load_pair(XS_BUFS)
+            copy_out(0, first[0][0], first[0][1], pts[0])
+            quantise(wq_in[:], ws_in[:], wg_in[:].rearrange("p c j -> p (c j)"))
+            for k in range(1, len(first)):
+                copy_out(0, first[k][0], first[k][1], pts[k])
+            quantise_x(0)
+            nc.vector.tensor_copy(out=sc[:], in_=sc_raw[:])
+            nc.vector.tensor_copy(out=bi[:], in_=bi_raw[:])
+
+            n_groups = len(GROUPS)
+            for gi in range(n_groups):
+                t0, w = span(gi)
+                nxt = GROUPS[gi + 1] if gi + 1 < n_groups else ()
+                banks = [(q, m) for q in nxt for m in range(3)]
+                passes = [(jp, m, jj) for jp in range(2) for m in range(3) for jj in range(2)]
+                per = len(banks) // 3
+                sq = {}
+                for k in range(3):
+                    part = banks[per * k : per * (k + 1)]
+                    pts = [transposes(q, m) for (q, m) in part]
+                    for q, m in part:
+                        if m == 2 and q + XS_BUFS < 8:
+                            load_pair(q + XS_BUFS)
+                    for jp, m, jj in passes[4 * k : 4 * k + 4]:
+                        j = 2 * jp + jj
+                        if jp not in sq:
+                            sq[jp] = qpool.tile([P, 3, 2, 512], F32, name="sq", tag="sq")
+                        h = ps_h.tile([P, 512], F32, name="h", tag="h")
+                        mx(
+                            h[:, :w],
+                            wq_in[:, P * j : P * (j + 1)],
+                            ws_in[:, P * j : P * (j + 1)],
+                            xq[:, m, t0 : t0 + w],
+                            xsc[:, m, t0 : t0 + w],
+                        )
+                        nc.scalar.activation(out=sq[jp][:, m, jj, :w], in_=h[:, :w], func=ACT.Square)
+                        eng = nc.vector if (gi, jp) in V_ADDS else nc.gpsimd
+                        if m == 1 and jj == 1:
+                            s01 = spool.tile([P, 2, 512], F32, name="s01", tag="s01")
+                            eng.tensor_tensor(
+                                out=s01[:, :, :w], in0=sq[jp][:, 0, :, :w], in1=sq[jp][:, 1, :, :w], op=ALU.add
+                            )
+                        if m == 2 and jj == 1:
+                            eng.tensor_tensor(
+                                out=a1[:, 2 * jp : 2 * jp + 2, t0 : t0 + w],
+                                in0=s01[:, :, :w],
+                                in1=sq[jp][:, 2, :, :w],
+                                op=ALU.add,
+                            )
+                    for i in range(len(part)):
+                        copy_out(gi + 1, part[i][0], part[i][1], pts[i])
+                if nxt:
+                    quantise_x(gi + 1)
+                else:
+                    nc.vector.tensor_copy(
+                        out=wg_out[:], in_=wr_out[:].rearrange("p j d -> p d j")
+                    )
+                if gi > 0:
+                    rsqrt(gi - 1, 0, 4)
+                    norm(gi - 1, 0, 4)
+            quantise(wq_out[:], ws_out[:], wg_out[:].rearrange("p c j -> p (c j)"))
+            for jp in range(2):
+                rsqrt(n_groups - 1, 2 * jp, 2 * jp + 2)
+                norm(n_groups - 1, 2 * jp, 2 * jp + 2)
+
+        with ExitStack() as bctx:
+            hpool = bctx.enter_context(tc.tile_pool(name="hpool", bufs=3))
+            opool = bctx.enter_context(tc.tile_pool(name="opool", bufs=6))
+            ps_b = bctx.enter_context(tc.psum_pool(name="ps_b", bufs=4))
+            ps_o = bctx.enter_context(tc.psum_pool(name="ps_o", bufs=4))
+
+            def gelu(gi, j):
+                t0, w = span(gi)
+                nc.scalar.activation(
+                    out=a1[:, j, t0 : t0 + w],
+                    in_=a1[:, j, t0 : t0 + w],
+                    func=ACT.Gelu,
+                    bias=bi[:, j : j + 1],
+                    scale=sc[:, j : j + 1],
+                )
+
+            def factor(c):
+                cols = slice(P * c, P * (c + 1))
+                nc.gpsimd.tensor_scalar(
+                    out=a2[:, :, cols], in0=a2[:, :, cols], scalar1=RN_MAX, scalar2=1.0, op0=ALU.min, op1=ALU.mult
+                )
+                nc.gpsimd.tensor_tensor(out=a2[:, :, cols], in0=a2[:, :, cols], in1=a1[:, :, cols], op=ALU.mult)
+
+            hbs = {}
+
+            def stage1b(c, m):
+                hb = ps_b.tile([P, 4, P], F32, name="hb", tag="hb")
+                hbs[(c, m)] = hb
+                for j in range(4):
+                    mx(
+                        hb[:, j, :],
+                        wq_in[:, P * j : P * (j + 1)],
+                        ws_in[:, P * j : P * (j + 1)],
+                        xq[:, m, P * c : P * (c + 1)],
+                        xsc[:, m, P * c : P * (c + 1)],
+                    )
+
+            late = [(gi, j) for gi in range(3, len(GROUPS)) for j in range(4)]
+            for gi in range(2):
+                for j in range(4):
+                    gelu(gi, j)
+            factor(0)
+            factor(1)
+            for j in range(4):
+                gelu(2, j)
+            for m in range(3):
+                stage1b(0, m)
+            for c in range(NCH):
+                if c + 1 < NCH:
+                    stage1b(c + 1, 0)
+                if c + 2 < NCH:
+                    factor(c + 2)
+                gg = hpool.tile([P, 3, P, 4], BF16, name="gg", tag="gg", align_bytes=64)
+                gq = hpool.tile([P, 3 * P], U32, name="gq", tag="gq", align_bytes=64)
+                gs = hpool.tile([P, 3 * P], U8, name="gs", tag="gs", align_bytes=64)
+                fac = a2[:, :, P * c : P * (c + 1)].rearrange("p j t -> p t j")
+                for m in range(3):
+                    nc.vector.tensor_tensor(
+                        out=gg[:, m, :, :], in0=hbs[(c, m)][:].rearrange("p j t -> p t j"), in1=fac, op=ALU.mult
+                    )
+                    if m < 2 and c + 1 < NCH:
+                        stage1b(c + 1, m + 1)
+                quantise(gq[:, 0 : 2 * P], gs[:, 0 : 2 * P], gg[:, 0:2, :, :].rearrange("p m t j -> p (m t j)"))
+                quantise(gq[:, 2 * P : 3 * P], gs[:, 2 * P : 3 * P], gg[:, 2, :, :].rearrange("p t j -> p (t j)"))
+                ot = opool.tile([P, E], F32, name="ot", tag="ot")
+                for dq in range(4):
+                    ob = ps_o.tile([P, 3, P], F32, name="ob", tag="ob")
+                    for m in range(3):
+                        mx(
+                            ob[:, m, :],
+                            gq[:, P * m : P * (m + 1)],
+                            gs[:, P * m : P * (m + 1)],
+                            wq_out[:, P * dq : P * (dq + 1)],
+                            ws_out[:, P * dq : P * (dq + 1)],
+                        )
+                    nc.scalar.copy(
+                        out=ot[:, 384 * dq : 384 * (dq + 1)].rearrange("p (d m) -> p d m", m=3),
+                        in_=ob[:].rearrange("p m d -> p d m"),
+                    )
+                nc.sync.dma_start(out=ov[:, c, :], in_=ot[:])
+                if c < len(late):
+                    gelu(late[c][0], late[c][1])

@@ -18,16 +18,16 @@ NCH = 16
 E = 1536
 TOK = 2048
 GROUPS = ((0,), (1,), (2, 3), (4, 5), (6, 7))
-S_COPIES = ((0, 1), (1, 1), (3, 1), (5, 1))
-V_ADDS = ()
+S_COPIES = ((0, 1), (1, 1), (2, 1), (3, 1), (4, 1), (5, 1), (6, 1), (7, 1))
+V_OUT = ((15, 1), (15, 3))
 XS_BUFS = 6
 RN_MAX = 1.0e12
 
 
 def tile_feedforwardse3_pa_t_kernel(tc, x, w_in, scale, bias, w_out, out):
     nc = tc.nc
-    xv = x.rearrange("b n d m -> (b n) (d m)").rearrange("(p c) e -> p c e", c=NCH)
-    ov = out.rearrange("b n d m -> (b n) (d m)").rearrange("(p c) e -> p c e", c=NCH)
+    xv = x.rearrange("b n (j d) m -> (b n j) (d m)", j=4).rearrange("(u p) e -> p u e", p=P)
+    ov = out.rearrange("b n d m -> (b n) (d m)").rearrange("(c p) e -> p c e", p=P)
 
     with ExitStack() as ctx:
         ctx.enter_context(tc.manual_schedule())
@@ -38,6 +38,8 @@ def tile_feedforwardse3_pa_t_kernel(tc, x, w_in, scale, bias, w_out, out):
         ws_in = keep.tile([P, 512], U8, name="ws_in", align_bytes=64)
         wq_out = keep.tile([P, 512], U32, name="wq_out", align_bytes=64)
         ws_out = keep.tile([P, 512], U8, name="ws_out", align_bytes=64)
+        wr_out = keep.tile([P, 4, 512], BF16, name="wr_out")
+        wg_out = keep.tile([P, 512, 4], BF16, name="wg_out", align_bytes=64)
         xq = keep.tile([P, 3, TOK], U32, name="xq", align_bytes=64)
         xsc = keep.tile([P, 3, TOK], U8, name="xsc", align_bytes=64)
         a1 = keep.tile([P, 4, TOK], F32, name="a1")
@@ -50,8 +52,8 @@ def tile_feedforwardse3_pa_t_kernel(tc, x, w_in, scale, bias, w_out, out):
         one2 = keep.tile([P, 1], F32, name="one2")
 
         def span(gi):
-            pairs = GROUPS[gi]
-            return 256 * pairs[0], 256 * len(pairs)
+            blocks = GROUPS[gi]
+            return 256 * blocks[0], 256 * len(blocks)
 
         def quantise(codes, scales, src):
             nc.vector.quantize_mx(out=codes.bitcast(FP8X4), scales=scales, in_=src)
@@ -70,33 +72,32 @@ def tile_feedforwardse3_pa_t_kernel(tc, x, w_in, scale, bias, w_out, out):
         with ExitStack() as actx:
             xpool = actx.enter_context(tc.tile_pool(name="xpool", bufs=XS_BUFS))
             gpool = actx.enter_context(tc.tile_pool(name="gpool", bufs=6))
-            qpool = actx.enter_context(tc.tile_pool(name="qpool", bufs=3))
-            spool = actx.enter_context(tc.tile_pool(name="spool", bufs=2))
+            qpool = actx.enter_context(tc.tile_pool(name="qpool", bufs=2))
             wpool = actx.enter_context(tc.tile_pool(name="wpool", bufs=1))
             ps_t = actx.enter_context(tc.psum_pool(name="ps_t", bufs=3))
             ps_h = actx.enter_context(tc.psum_pool(name="ps_h", bufs=5))
 
             xs = {}
             xg = {}
+            sq = {}
 
-            def load_pair(q):
-                xs[q] = xpool.tile([P, 2, E], BF16, name="xs", tag="xs")
-                nc.sync.dma_start(out=xs[q][:], in_=xv[:, 2 * q : 2 * q + 2, :])
+            def load_block(q):
+                xs[q] = xpool.tile([P, 8, 384], BF16, name="xs", tag="xs")
+                nc.sync.dma_start(out=xs[q][:], in_=xv[:, 8 * q : 8 * q + 8, :])
 
             def transposes(q, m):
-                pt = ps_t.tile([P, 2, 4, P], BF16, name="pt", tag="pt")
-                for u in range(2):
+                pt = ps_t.tile([P, 8, P], BF16, name="pt", tag="pt")
+                for u in range(8):
                     src = xs[q][:, u, :].rearrange("p (d m) -> p d m", m=3)
-                    for j in range(4):
-                        nc.tensor.transpose(pt[:, u, j, :], src[:, P * j : P * (j + 1), m], ident[:])
+                    nc.tensor.transpose(pt[:, u, :], src[:, :, m], ident[:])
                 return pt
 
             def copy_out(gi, q, m, pt):
                 if (gi, m) not in xg:
-                    xg[(gi, m)] = gpool.tile([P, 512, 4], BF16, name="xg", tag="xg", align_bytes=64)
+                    xg[(gi, m)] = gpool.tile([P, 2048], BF16, name="xg", tag="xg", align_bytes=64)
                 h = q - GROUPS[gi][0]
-                dst = xg[(gi, m)][:, 256 * h : 256 * (h + 1), :].rearrange("p (c t) j -> p c t j", c=2)
-                src = pt[:].rearrange("p c j t -> p c t j")
+                dst = xg[(gi, m)][:, 1024 * h : 1024 * (h + 1)]
+                src = pt[:].rearrange("p u c -> p (u c)")
                 if (q, m) in S_COPIES:
                     nc.scalar.copy(out=dst, in_=src)
                 else:
@@ -105,11 +106,19 @@ def tile_feedforwardse3_pa_t_kernel(tc, x, w_in, scale, bias, w_out, out):
             def quantise_x(gi):
                 t0, w = span(gi)
                 for m in range(3):
-                    quantise(
-                        xq[:, m, t0 : t0 + w],
-                        xsc[:, m, t0 : t0 + w],
-                        xg[(gi, m)][:, :w, :].rearrange("p c j -> p (c j)"),
-                    )
+                    quantise(xq[:, m, t0 : t0 + w], xsc[:, m, t0 : t0 + w], xg[(gi, m)][:, : 4 * w])
+
+            def add1(gi):
+                t0, w = span(gi)
+                nc.vector.tensor_tensor(
+                    out=sq[gi][:, 0, :, :w], in0=sq[gi][:, 0, :, :w], in1=sq[gi][:, 1, :, :w], op=ALU.add
+                )
+
+            def add2(gi, j0, j1):
+                t0, w = span(gi)
+                nc.vector.tensor_tensor(
+                    out=a1[:, j0:j1, t0 : t0 + w], in0=sq[gi][:, 0, j0:j1, :w], in1=sq[gi][:, 2, j0:j1, :w], op=ALU.add
+                )
 
             def rsqrt(gi, j0, j1):
                 t0, w = span(gi)
@@ -130,17 +139,15 @@ def tile_feedforwardse3_pa_t_kernel(tc, x, w_in, scale, bias, w_out, out):
 
             wr_in = wpool.tile([P, 4, 512], BF16, name="wr_in")
             wg_in = wpool.tile([P, 512, 4], BF16, name="wg_in", align_bytes=64)
-            wr_out = wpool.tile([P, 4, 512], BF16, name="wr_out")
-            wg_out = wpool.tile([P, 512, 4], BF16, name="wg_out", align_bytes=64)
             nc.scalar.dma_start(out=wr_in[:], in_=w_in.rearrange("(j p) f -> p j f", p=P))
-            load_pair(0)
+            load_block(0)
             nc.scalar.dma_start(out=sc_raw[:], in_=scale.rearrange("a b (p j) -> (a b p) j", j=4))
             nc.scalar.dma_start(out=bi_raw[:], in_=bias.rearrange("a b (p j) -> (a b p) j", j=4))
             make_identity(nc, ident[:])
             nc.vector.memset(one[:], 1.0)
             nc.scalar.activation(out=one2[:], in_=one[:], func=ACT.Abs_reciprocal_sqrt)
             for q in range(1, XS_BUFS):
-                load_pair(q)
+                load_block(q)
             nc.sync.dma_start(out=wr_out[:], in_=w_out.rearrange("(p j) d -> p j d", j=4))
 
             wsrc = wr_in[:].rearrange("p j (b a) -> p a b j", a=4)
@@ -150,33 +157,32 @@ def tile_feedforwardse3_pa_t_kernel(tc, x, w_in, scale, bias, w_out, out):
 
             first = [(q, m) for q in GROUPS[0] for m in range(3)]
             pts = [transposes(q, m) for (q, m) in first]
-            load_pair(XS_BUFS)
+            load_block(XS_BUFS)
             copy_out(0, first[0][0], first[0][1], pts[0])
             quantise(wq_in[:], ws_in[:], wg_in[:].rearrange("p c j -> p (c j)"))
             for k in range(1, len(first)):
                 copy_out(0, first[k][0], first[k][1], pts[k])
             quantise_x(0)
-            nc.vector.tensor_copy(out=sc[:], in_=sc_raw[:])
-            nc.vector.tensor_copy(out=bi[:], in_=bi_raw[:])
+            nc.scalar.copy(out=sc[:], in_=sc_raw[:])
+            nc.scalar.copy(out=bi[:], in_=bi_raw[:])
 
             n_groups = len(GROUPS)
             for gi in range(n_groups):
                 t0, w = span(gi)
-                nxt = GROUPS[gi + 1] if gi + 1 < n_groups else ()
+                last = gi == n_groups - 1
+                nxt = () if last else GROUPS[gi + 1]
                 banks = [(q, m) for q in nxt for m in range(3)]
-                passes = [(jp, m, jj) for jp in range(2) for m in range(3) for jj in range(2)]
                 per = len(banks) // 3
-                sq = {}
-                for k in range(3):
-                    part = banks[per * k : per * (k + 1)]
-                    pts = [transposes(q, m) for (q, m) in part]
-                    for q, m in part:
-                        if m == 2 and q + XS_BUFS < 8:
-                            load_pair(q + XS_BUFS)
-                    for jp, m, jj in passes[4 * k : 4 * k + 4]:
-                        j = 2 * jp + jj
-                        if jp not in sq:
-                            sq[jp] = qpool.tile([P, 3, 2, 512], F32, name="sq", tag="sq")
+                if gi > 0:
+                    add2(gi - 1, 0, 4)
+                sq[gi] = qpool.tile([P, 3, 4, 512], F32, name="sq", tag="sq")
+                for m in range(3):
+                    part = banks[per * m : per * (m + 1)]
+                    pts = [transposes(q, mm) for (q, mm) in part]
+                    for q, mm in part:
+                        if mm == 2 and q + XS_BUFS < 8:
+                            load_block(q + XS_BUFS)
+                    for j in range(4):
                         h = ps_h.tile([P, 512], F32, name="h", tag="h")
                         mx(
                             h[:, :w],
@@ -185,34 +191,23 @@ def tile_feedforwardse3_pa_t_kernel(tc, x, w_in, scale, bias, w_out, out):
                             xq[:, m, t0 : t0 + w],
                             xsc[:, m, t0 : t0 + w],
                         )
-                        nc.scalar.activation(out=sq[jp][:, m, jj, :w], in_=h[:, :w], func=ACT.Square)
-                        eng = nc.vector if (gi, jp) in V_ADDS else nc.gpsimd
-                        if m == 1 and jj == 1:
-                            s01 = spool.tile([P, 2, 512], F32, name="s01", tag="s01")
-                            eng.tensor_tensor(
-                                out=s01[:, :, :w], in0=sq[jp][:, 0, :, :w], in1=sq[jp][:, 1, :, :w], op=ALU.add
-                            )
-                        if m == 2 and jj == 1:
-                            eng.tensor_tensor(
-                                out=a1[:, 2 * jp : 2 * jp + 2, t0 : t0 + w],
-                                in0=s01[:, :, :w],
-                                in1=sq[jp][:, 2, :, :w],
-                                op=ALU.add,
-                            )
+                        nc.scalar.activation(out=sq[gi][:, m, j, :w], in_=h[:, :w], func=ACT.Square)
                     for i in range(len(part)):
                         copy_out(gi + 1, part[i][0], part[i][1], pts[i])
-                if nxt:
-                    quantise_x(gi + 1)
-                else:
-                    nc.vector.tensor_copy(
-                        out=wg_out[:], in_=wr_out[:].rearrange("p j d -> p d j")
-                    )
-                if gi > 0:
+                    if m == 1:
+                        add1(gi)
+                        if gi > 0 and not last:
+                            rsqrt(gi - 1, 0, 4)
+                if last:
                     rsqrt(gi - 1, 0, 4)
+                else:
+                    quantise_x(gi + 1)
+                if gi > 0:
                     norm(gi - 1, 0, 4)
-            quantise(wq_out[:], ws_out[:], wg_out[:].rearrange("p c j -> p (c j)"))
             for jp in range(2):
+                add2(n_groups - 1, 2 * jp, 2 * jp + 2)
                 rsqrt(n_groups - 1, 2 * jp, 2 * jp + 2)
+            for jp in range(2):
                 norm(n_groups - 1, 2 * jp, 2 * jp + 2)
 
         with ExitStack() as bctx:
@@ -231,12 +226,11 @@ def tile_feedforwardse3_pa_t_kernel(tc, x, w_in, scale, bias, w_out, out):
                     scale=sc[:, j : j + 1],
                 )
 
-            def factor(c):
-                cols = slice(P * c, P * (c + 1))
-                nc.gpsimd.tensor_scalar(
-                    out=a2[:, :, cols], in0=a2[:, :, cols], scalar1=RN_MAX, scalar2=1.0, op0=ALU.min, op1=ALU.mult
+            def factor(b):
+                cols = slice(256 * b, 256 * (b + 1))
+                nc.vector.scalar_tensor_tensor(
+                    out=a2[:, :, cols], in0=a2[:, :, cols], scalar=RN_MAX, in1=a1[:, :, cols], op0=ALU.min, op1=ALU.mult
                 )
-                nc.gpsimd.tensor_tensor(out=a2[:, :, cols], in0=a2[:, :, cols], in1=a1[:, :, cols], op=ALU.mult)
 
             hbs = {}
 
@@ -253,20 +247,19 @@ def tile_feedforwardse3_pa_t_kernel(tc, x, w_in, scale, bias, w_out, out):
                     )
 
             late = [(gi, j) for gi in range(3, len(GROUPS)) for j in range(4)]
-            for gi in range(2):
-                for j in range(4):
-                    gelu(gi, j)
-            factor(0)
-            factor(1)
-            for j in range(4):
-                gelu(2, j)
             for m in range(3):
                 stage1b(0, m)
+            for j in range(4):
+                gelu(0, j)
+            factor(0)
+            for j in range(4):
+                gelu(1, j)
+            nc.scalar.copy(out=wg_out[:], in_=wr_out[:].rearrange("p j d -> p d j"))
+            for j in range(4):
+                gelu(2, j)
             for c in range(NCH):
                 if c + 1 < NCH:
                     stage1b(c + 1, 0)
-                if c + 2 < NCH:
-                    factor(c + 2)
                 gg = hpool.tile([P, 3, P, 4], BF16, name="gg", tag="gg", align_bytes=64)
                 gq = hpool.tile([P, 3 * P], U32, name="gq", tag="gq", align_bytes=64)
                 gs = hpool.tile([P, 3 * P], U8, name="gs", tag="gs", align_bytes=64)
@@ -279,6 +272,10 @@ def tile_feedforwardse3_pa_t_kernel(tc, x, w_in, scale, bias, w_out, out):
                         stage1b(c + 1, m + 1)
                 quantise(gq[:, 0 : 2 * P], gs[:, 0 : 2 * P], gg[:, 0:2, :, :].rearrange("p m t j -> p (m t j)"))
                 quantise(gq[:, 2 * P : 3 * P], gs[:, 2 * P : 3 * P], gg[:, 2, :, :].rearrange("p t j -> p (t j)"))
+                if c == 0:
+                    quantise(wq_out[:], ws_out[:], wg_out[:].rearrange("p c j -> p (c j)"))
+                if c % 2 == 0 and c // 2 + 1 < 8:
+                    factor(c // 2 + 1)
                 ot = opool.tile([P, E], F32, name="ot", tag="ot")
                 for dq in range(4):
                     ob = ps_o.tile([P, 3, P], F32, name="ob", tag="ob")
@@ -290,10 +287,17 @@ def tile_feedforwardse3_pa_t_kernel(tc, x, w_in, scale, bias, w_out, out):
                             wq_out[:, P * dq : P * (dq + 1)],
                             ws_out[:, P * dq : P * (dq + 1)],
                         )
-                    nc.scalar.copy(
-                        out=ot[:, 384 * dq : 384 * (dq + 1)].rearrange("p (d m) -> p d m", m=3),
-                        in_=ob[:].rearrange("p m d -> p d m"),
-                    )
-                nc.sync.dma_start(out=ov[:, c, :], in_=ot[:])
+                    dst = ot[:, 384 * dq : 384 * (dq + 1)].rearrange("p (d m) -> p d m", m=3)
+                    src = ob[:].rearrange("p m d -> p d m")
+                    if (c, dq) in V_OUT:
+                        nc.vector.tensor_copy(out=dst, in_=src)
+                    else:
+                        nc.scalar.copy(out=dst, in_=src)
+                    if c == NCH - 1 and dq == 1:
+                        nc.sync.dma_start(out=ov[:, c, 0:768], in_=ot[:, 0:768])
+                if c == NCH - 1:
+                    nc.sync.dma_start(out=ov[:, c, 768:E], in_=ot[:, 768:E])
+                else:
+                    nc.sync.dma_start(out=ov[:, c, :], in_=ot[:])
                 if c < len(late):
                     gelu(late[c][0], late[c][1])

@@ -15,25 +15,27 @@ ALU = mybir.AluOpType
 
 P = 128
 NCH = 16
+NB = 8
+BT = 256
 E = 1536
 TOK = 2048
-GROUPS = ((0,), (1,), (2, 3), (4, 5), (6, 7))
-S_COPIES = ((0, 1), (1, 1), (2, 1), (3, 1), (4, 1), (5, 1), (6, 1), (7, 1))
+LA = 5
+V_COPIES = ()
 V_OUT = ((15, 1), (15, 3))
-XS_BUFS = 6
+XS_BUFS = 4
 RN_MAX = 1.0e12
 
 
 def tile_feedforwardse3_pa_t_kernel(tc, x, w_in, scale, bias, w_out, out):
     nc = tc.nc
-    xv = x.rearrange("b n (j d) m -> (b n j) (d m)", j=4).rearrange("(u p) e -> p u e", p=P)
+    xv = x.rearrange("b n (h d) m -> (b n h) (d m)", h=2).rearrange("(u p) e -> p u e", p=P)
     ov = out.rearrange("b n d m -> (b n) (d m)").rearrange("(c p) e -> p c e", p=P)
 
     with ExitStack() as ctx:
         ctx.enter_context(tc.manual_schedule())
         keep = ctx.enter_context(tc.tile_pool(name="keep", bufs=1))
 
-        ident = keep.tile([P, P], BF16, name="ident")
+        ident = keep.tile([P, P], F32, name="ident")
         wq_in = keep.tile([P, 512], U32, name="wq_in", align_bytes=64)
         ws_in = keep.tile([P, 512], U8, name="ws_in", align_bytes=64)
         wq_out = keep.tile([P, 512], U32, name="wq_out", align_bytes=64)
@@ -51,10 +53,6 @@ def tile_feedforwardse3_pa_t_kernel(tc, x, w_in, scale, bias, w_out, out):
         one = keep.tile([P, 1], F32, name="one")
         one2 = keep.tile([P, 1], F32, name="one2")
 
-        def span(gi):
-            blocks = GROUPS[gi]
-            return 256 * blocks[0], 256 * len(blocks)
-
         def quantise(codes, scales, src):
             nc.vector.quantize_mx(out=codes.bitcast(FP8X4), scales=scales, in_=src)
 
@@ -71,144 +69,148 @@ def tile_feedforwardse3_pa_t_kernel(tc, x, w_in, scale, bias, w_out, out):
 
         with ExitStack() as actx:
             xpool = actx.enter_context(tc.tile_pool(name="xpool", bufs=XS_BUFS))
-            gpool = actx.enter_context(tc.tile_pool(name="gpool", bufs=6))
-            qpool = actx.enter_context(tc.tile_pool(name="qpool", bufs=2))
+            dpool = actx.enter_context(tc.tile_pool(name="dpool", bufs=3))
+            gpool = actx.enter_context(tc.tile_pool(name="gpool", bufs=3))
+            qpool = actx.enter_context(tc.tile_pool(name="qpool", bufs=3))
             wpool = actx.enter_context(tc.tile_pool(name="wpool", bufs=1))
             ps_t = actx.enter_context(tc.psum_pool(name="ps_t", bufs=3))
-            ps_h = actx.enter_context(tc.psum_pool(name="ps_h", bufs=5))
+            ps_h = actx.enter_context(tc.psum_pool(name="ps_h", bufs=LA))
 
             xs = {}
+            xd = {}
             xg = {}
             sq = {}
+            pts = {}
+            hh = {}
 
-            def load_block(q):
-                xs[q] = xpool.tile([P, 8, 384], BF16, name="xs", tag="xs")
-                nc.sync.dma_start(out=xs[q][:], in_=xv[:, 8 * q : 8 * q + 8, :])
+            def ok(b):
+                return 0 <= b < NB
 
-            def transposes(q, m):
-                pt = ps_t.tile([P, 8, P], BF16, name="pt", tag="pt")
-                for u in range(8):
-                    src = xs[q][:, u, :].rearrange("p (d m) -> p d m", m=3)
-                    nc.tensor.transpose(pt[:, u, :], src[:, :, m], ident[:])
-                return pt
+            def load_block(b):
+                xs[b] = xpool.tile([P, 4, 768], BF16, name="xs", tag="xs")
+                nc.sync.dma_start(out=xs[b][:], in_=xv[:, 4 * b : 4 * b + 4, :])
 
-            def copy_out(gi, q, m, pt):
-                if (gi, m) not in xg:
-                    xg[(gi, m)] = gpool.tile([P, 2048], BF16, name="xg", tag="xg", align_bytes=64)
-                h = q - GROUPS[gi][0]
-                dst = xg[(gi, m)][:, 1024 * h : 1024 * (h + 1)]
-                src = pt[:].rearrange("p u c -> p (u c)")
-                if (q, m) in S_COPIES:
-                    nc.scalar.copy(out=dst, in_=src)
-                else:
+            def deinterleave(b, m):
+                if m == 0:
+                    xd[b] = dpool.tile([P, 3, 4, BT], BF16, name="xd", tag="xd")
+                src = xs[b][:].rearrange("p u (d m) -> p m u d", m=3)
+                nc.vector.tensor_copy(out=xd[b][:, m, :, :], in_=src[:, m, :, :])
+
+            def transposes(b, m):
+                pts[(b, m)] = ps_t.tile([P, 4, P], F32, name="pt", tag="pt")
+                for u in range(4):
+                    nc.tensor.transpose(pts[(b, m)][:, u, :], xd[b][:, m, u, :].bitcast(F32), ident[:])
+
+            def copy_out(b, m):
+                if m == 0:
+                    xg[b] = gpool.tile([P, 3, 4 * BT], BF16, name="xg", tag="xg", align_bytes=64)
+                dst = xg[b][:, m, :].bitcast(F32)
+                src = pts[(b, m)][:].rearrange("p u c -> p (u c)")
+                if (b, m) in V_COPIES:
                     nc.vector.tensor_copy(out=dst, in_=src)
+                else:
+                    nc.scalar.copy(out=dst, in_=src)
 
-            def quantise_x(gi):
-                t0, w = span(gi)
-                for m in range(3):
-                    quantise(xq[:, m, t0 : t0 + w], xsc[:, m, t0 : t0 + w], xg[(gi, m)][:, : 4 * w])
+            def quantise_x(b, m):
+                cols = slice(BT * b, BT * (b + 1))
+                quantise(xq[:, m, cols], xsc[:, m, cols], xg[b][:, m, :])
 
-            def add1(gi):
-                t0, w = span(gi)
-                nc.vector.tensor_tensor(
-                    out=sq[gi][:, 0, :, :w], in0=sq[gi][:, 0, :, :w], in1=sq[gi][:, 1, :, :w], op=ALU.add
-                )
+            def stage1a(n):
+                b, i = divmod(n, 6)
+                m, jp = divmod(i, 2)
+                cols = slice(BT * b, BT * (b + 1))
+                hh[n] = ps_h.tile([P, 2, BT], F32, name="hh", tag="hh")
+                for jj in range(2):
+                    j = 2 * jp + jj
+                    mx(
+                        hh[n][:, jj, :],
+                        wq_in[:, P * j : P * (j + 1)],
+                        ws_in[:, P * j : P * (j + 1)],
+                        xq[:, m, cols],
+                        xsc[:, m, cols],
+                    )
 
-            def add2(gi, j0, j1):
-                t0, w = span(gi)
-                nc.vector.tensor_tensor(
-                    out=a1[:, j0:j1, t0 : t0 + w], in0=sq[gi][:, 0, j0:j1, :w], in1=sq[gi][:, 2, j0:j1, :w], op=ALU.add
-                )
+            def square(n):
+                b, i = divmod(n, 6)
+                m, jp = divmod(i, 2)
+                if i == 0:
+                    sq[b] = qpool.tile([P, 3, 4, BT], F32, name="sq", tag="sq")
+                nc.scalar.activation(out=sq[b][:, m, 2 * jp : 2 * jp + 2, :], in_=hh[n][:], func=ACT.Square)
 
-            def rsqrt(gi, j0, j1):
-                t0, w = span(gi)
-                nc.scalar.activation(
-                    out=a2[:, j0:j1, t0 : t0 + w], in_=a1[:, j0:j1, t0 : t0 + w], func=ACT.Abs_reciprocal_sqrt
-                )
+            def add1(b):
+                nc.vector.tensor_tensor(out=sq[b][:, 0, :, :], in0=sq[b][:, 0, :, :], in1=sq[b][:, 1, :, :], op=ALU.add)
 
-            def norm(gi, j0, j1):
-                t0, w = span(gi)
+            def add2(b):
+                cols = slice(BT * b, BT * (b + 1))
+                nc.vector.tensor_tensor(out=a1[:, :, cols], in0=sq[b][:, 0, :, :], in1=sq[b][:, 2, :, :], op=ALU.add)
+
+            def rsqrt(b):
+                cols = slice(BT * b, BT * (b + 1))
+                nc.scalar.activation(out=a2[:, :, cols], in_=a1[:, :, cols], func=ACT.Abs_reciprocal_sqrt)
+
+            def norm(b):
+                cols = slice(BT * b, BT * (b + 1))
                 nc.vector.scalar_tensor_tensor(
-                    out=a1[:, j0:j1, t0 : t0 + w],
-                    in0=a2[:, j0:j1, t0 : t0 + w],
-                    scalar=RN_MAX,
-                    in1=a1[:, j0:j1, t0 : t0 + w],
-                    op0=ALU.min,
-                    op1=ALU.mult,
+                    out=a1[:, :, cols], in0=a2[:, :, cols], scalar=RN_MAX, in1=a1[:, :, cols], op0=ALU.min, op1=ALU.mult
                 )
 
             wr_in = wpool.tile([P, 4, 512], BF16, name="wr_in")
             wg_in = wpool.tile([P, 512, 4], BF16, name="wg_in", align_bytes=64)
-            nc.scalar.dma_start(out=wr_in[:], in_=w_in.rearrange("(j p) f -> p j f", p=P))
+            nc.scalar.dma_start(
+                out=wr_in[:].rearrange("p (h e) f -> p h (e f)", h=2),
+                in_=w_in.rearrange("(h a e) f -> a h (e f)", h=2, e=2),
+            )
             load_block(0)
             nc.scalar.dma_start(out=sc_raw[:], in_=scale.rearrange("a b (p j) -> (a b p) j", j=4))
             nc.scalar.dma_start(out=bi_raw[:], in_=bias.rearrange("a b (p j) -> (a b p) j", j=4))
             make_identity(nc, ident[:])
             nc.vector.memset(one[:], 1.0)
             nc.scalar.activation(out=one2[:], in_=one[:], func=ACT.Abs_reciprocal_sqrt)
-            for q in range(1, XS_BUFS):
-                load_block(q)
-            nc.sync.dma_start(out=wr_out[:], in_=w_out.rearrange("(p j) d -> p j d", j=4))
+            for b in range(1, XS_BUFS):
+                load_block(b)
 
             wsrc = wr_in[:].rearrange("p j (b a) -> p a b j", a=4)
             wdst = wg_in[:].rearrange("p (a b) j -> p a b j", a=4)
             nc.vector.tensor_copy(out=wdst[:, 0:2, :, :], in_=wsrc[:, 0:2, :, :])
             nc.scalar.copy(out=wdst[:, 2:4, :, :], in_=wsrc[:, 2:4, :, :])
-
-            first = [(q, m) for q in GROUPS[0] for m in range(3)]
-            pts = [transposes(q, m) for (q, m) in first]
-            load_block(XS_BUFS)
-            copy_out(0, first[0][0], first[0][1], pts[0])
-            quantise(wq_in[:], ws_in[:], wg_in[:].rearrange("p c j -> p (c j)"))
-            for k in range(1, len(first)):
-                copy_out(0, first[k][0], first[k][1], pts[k])
-            quantise_x(0)
             nc.scalar.copy(out=sc[:], in_=sc_raw[:])
             nc.scalar.copy(out=bi[:], in_=bi_raw[:])
 
-            n_groups = len(GROUPS)
-            for gi in range(n_groups):
-                t0, w = span(gi)
-                last = gi == n_groups - 1
-                nxt = () if last else GROUPS[gi + 1]
-                banks = [(q, m) for q in nxt for m in range(3)]
-                per = len(banks) // 3
-                if gi > 0:
-                    add2(gi - 1, 0, 4)
-                sq[gi] = qpool.tile([P, 3, 4, 512], F32, name="sq", tag="sq")
-                for m in range(3):
-                    part = banks[per * m : per * (m + 1)]
-                    pts = [transposes(q, mm) for (q, mm) in part]
-                    for q, mm in part:
-                        if mm == 2 and q + XS_BUFS < 8:
-                            load_block(q + XS_BUFS)
-                    for j in range(4):
-                        h = ps_h.tile([P, 512], F32, name="h", tag="h")
-                        mx(
-                            h[:, :w],
-                            wq_in[:, P * j : P * (j + 1)],
-                            ws_in[:, P * j : P * (j + 1)],
-                            xq[:, m, t0 : t0 + w],
-                            xsc[:, m, t0 : t0 + w],
-                        )
-                        nc.scalar.activation(out=sq[gi][:, m, j, :w], in_=h[:, :w], func=ACT.Square)
-                    for i in range(len(part)):
-                        copy_out(gi + 1, part[i][0], part[i][1], pts[i])
-                    if m == 1:
-                        add1(gi)
-                        if gi > 0 and not last:
-                            rsqrt(gi - 1, 0, 4)
-                if last:
-                    rsqrt(gi - 1, 0, 4)
-                else:
-                    quantise_x(gi + 1)
-                if gi > 0:
-                    norm(gi - 1, 0, 4)
-            for jp in range(2):
-                add2(n_groups - 1, 2 * jp, 2 * jp + 2)
-                rsqrt(n_groups - 1, 2 * jp, 2 * jp + 2)
-            for jp in range(2):
-                norm(n_groups - 1, 2 * jp, 2 * jp + 2)
+            for s in range(-2, NB + 2):
+                for i in range(6):
+                    n = 6 * s + i
+                    if i == 0 and ok(s - 1):
+                        add2(s - 1)
+                    if i == 0 and ok(s - 2) and s - 2 < NB - 2:
+                        norm(s - 2)
+                    if 1 <= i <= 3 and ok(s + 1):
+                        quantise_x(s + 1, i - 1)
+                    if 1 <= i <= 3 and ok(s + 2):
+                        deinterleave(s + 2, i - 1)
+                        if s + 2 == 0 and i == 2:
+                            quantise(wq_in[:], ws_in[:], wg_in[:].rearrange("p c j -> p (c j)"))
+                        if i == 3 and s + 2 + XS_BUFS < NB:
+                            load_block(s + 2 + XS_BUFS)
+                        if i == 3 and s + 2 == NB - 1:
+                            nc.sync.dma_start(out=wr_out[:], in_=w_out.rearrange("(p j) d -> p j d", j=4))
+                    if i == 4 and ok(s):
+                        add1(s)
+                    if 0 <= n < 6 * NB:
+                        square(n)
+                    if 0 <= n + LA < 6 * NB:
+                        stage1a(n + LA)
+                    if i < 3 and ok(s + 1):
+                        copy_out(s + 1, i)
+                    if 1 <= i <= 3 and ok(s + 2):
+                        transposes(s + 2, i - 1)
+                    if i == 3 and ok(s - 1) and s - 1 < NB - 2:
+                        rsqrt(s - 1)
+            rsqrt(NB - 2)
+            norm(NB - 2)
+            rsqrt(NB - 1)
+            nc.vector.tensor_copy(out=wg_out[:], in_=wr_out[:].rearrange("p j d -> p d j"))
+            norm(NB - 1)
+            quantise(wq_out[:], ws_out[:], wg_out[:].rearrange("p c j -> p (c j)"))
 
         with ExitStack() as bctx:
             hpool = bctx.enter_context(tc.tile_pool(name="hpool", bufs=3))
@@ -216,8 +218,7 @@ def tile_feedforwardse3_pa_t_kernel(tc, x, w_in, scale, bias, w_out, out):
             ps_b = bctx.enter_context(tc.psum_pool(name="ps_b", bufs=4))
             ps_o = bctx.enter_context(tc.psum_pool(name="ps_o", bufs=4))
 
-            def gelu(gi, j):
-                t0, w = span(gi)
+            def gelu(t0, w, j):
                 nc.scalar.activation(
                     out=a1[:, j, t0 : t0 + w],
                     in_=a1[:, j, t0 : t0 + w],
@@ -226,8 +227,8 @@ def tile_feedforwardse3_pa_t_kernel(tc, x, w_in, scale, bias, w_out, out):
                     scale=sc[:, j : j + 1],
                 )
 
-            def factor(b):
-                cols = slice(256 * b, 256 * (b + 1))
+            def factor(t0, w):
+                cols = slice(t0, t0 + w)
                 nc.vector.scalar_tensor_tensor(
                     out=a2[:, :, cols], in0=a2[:, :, cols], scalar=RN_MAX, in1=a1[:, :, cols], op0=ALU.min, op1=ALU.mult
                 )
@@ -246,17 +247,14 @@ def tile_feedforwardse3_pa_t_kernel(tc, x, w_in, scale, bias, w_out, out):
                         xsc[:, m, P * c : P * (c + 1)],
                     )
 
-            late = [(gi, j) for gi in range(3, len(GROUPS)) for j in range(4)]
+            late = [(t0, j) for t0 in (1024, 1536) for j in range(4)]
             for m in range(3):
                 stage1b(0, m)
-            for j in range(4):
-                gelu(0, j)
-            factor(0)
-            for j in range(4):
-                gelu(1, j)
-            nc.scalar.copy(out=wg_out[:], in_=wr_out[:].rearrange("p j d -> p d j"))
-            for j in range(4):
-                gelu(2, j)
+            for t0, w in ((0, 128), (128, 128), (256, 256), (512, 512)):
+                for j in range(4):
+                    gelu(t0, w, j)
+                if t0 == 0:
+                    factor(0, 128)
             for c in range(NCH):
                 if c + 1 < NCH:
                     stage1b(c + 1, 0)
@@ -273,9 +271,9 @@ def tile_feedforwardse3_pa_t_kernel(tc, x, w_in, scale, bias, w_out, out):
                 quantise(gq[:, 0 : 2 * P], gs[:, 0 : 2 * P], gg[:, 0:2, :, :].rearrange("p m t j -> p (m t j)"))
                 quantise(gq[:, 2 * P : 3 * P], gs[:, 2 * P : 3 * P], gg[:, 2, :, :].rearrange("p t j -> p (t j)"))
                 if c == 0:
-                    quantise(wq_out[:], ws_out[:], wg_out[:].rearrange("p c j -> p (c j)"))
-                if c % 2 == 0 and c // 2 + 1 < 8:
-                    factor(c // 2 + 1)
+                    factor(128, 128)
+                if c % 2 == 0 and c // 2 + 1 < NB:
+                    factor(BT * (c // 2 + 1), BT)
                 ot = opool.tile([P, E], F32, name="ot", tag="ot")
                 for dq in range(4):
                     ob = ps_o.tile([P, 3, P], F32, name="ob", tag="ob")
@@ -300,4 +298,4 @@ def tile_feedforwardse3_pa_t_kernel(tc, x, w_in, scale, bias, w_out, out):
                 else:
                     nc.sync.dma_start(out=ov[:, c, :], in_=ot[:])
                 if c < len(late):
-                    gelu(late[c][0], late[c][1])
+                    gelu(late[c][0], 512, late[c][1])

@@ -20,7 +20,7 @@ BT = 256
 E = 1536
 TOK = 2048
 LA = 5
-V_COPIES = ()
+V_COPY_M = (0, 2)
 V_OUT = ((15, 1), (15, 3))
 XS_BUFS = 4
 RN_MAX = 1.0e12
@@ -28,14 +28,14 @@ RN_MAX = 1.0e12
 
 def tile_feedforwardse3_pa_t_kernel(tc, x, w_in, scale, bias, w_out, out):
     nc = tc.nc
-    xv = x.rearrange("b n (h d) m -> (b n h) (d m)", h=2).rearrange("(u p) e -> p u e", p=P)
+    xv = x.rearrange("b n (j d) m -> (b n j) (d m)", j=4).rearrange("(u p) e -> p u e", p=P)
     ov = out.rearrange("b n d m -> (b n) (d m)").rearrange("(c p) e -> p c e", p=P)
 
     with ExitStack() as ctx:
         ctx.enter_context(tc.manual_schedule())
         keep = ctx.enter_context(tc.tile_pool(name="keep", bufs=1))
 
-        ident = keep.tile([P, P], F32, name="ident")
+        ident = keep.tile([P, P], BF16, name="ident")
         wq_in = keep.tile([P, 512], U32, name="wq_in", align_bytes=64)
         ws_in = keep.tile([P, 512], U8, name="ws_in", align_bytes=64)
         wq_out = keep.tile([P, 512], U32, name="wq_out", align_bytes=64)
@@ -69,7 +69,6 @@ def tile_feedforwardse3_pa_t_kernel(tc, x, w_in, scale, bias, w_out, out):
 
         with ExitStack() as actx:
             xpool = actx.enter_context(tc.tile_pool(name="xpool", bufs=XS_BUFS))
-            dpool = actx.enter_context(tc.tile_pool(name="dpool", bufs=3))
             gpool = actx.enter_context(tc.tile_pool(name="gpool", bufs=3))
             qpool = actx.enter_context(tc.tile_pool(name="qpool", bufs=3))
             wpool = actx.enter_context(tc.tile_pool(name="wpool", bufs=1))
@@ -77,7 +76,6 @@ def tile_feedforwardse3_pa_t_kernel(tc, x, w_in, scale, bias, w_out, out):
             ps_h = actx.enter_context(tc.psum_pool(name="ps_h", bufs=LA))
 
             xs = {}
-            xd = {}
             xg = {}
             sq = {}
             pts = {}
@@ -87,26 +85,21 @@ def tile_feedforwardse3_pa_t_kernel(tc, x, w_in, scale, bias, w_out, out):
                 return 0 <= b < NB
 
             def load_block(b):
-                xs[b] = xpool.tile([P, 4, 768], BF16, name="xs", tag="xs")
-                nc.sync.dma_start(out=xs[b][:], in_=xv[:, 4 * b : 4 * b + 4, :])
-
-            def deinterleave(b, m):
-                if m == 0:
-                    xd[b] = dpool.tile([P, 3, 4, BT], BF16, name="xd", tag="xd")
-                src = xs[b][:].rearrange("p u (d m) -> p m u d", m=3)
-                nc.vector.tensor_copy(out=xd[b][:, m, :, :], in_=src[:, m, :, :])
+                xs[b] = xpool.tile([P, 8, 384], BF16, name="xs", tag="xs")
+                nc.sync.dma_start(out=xs[b][:], in_=xv[:, 8 * b : 8 * b + 8, :])
 
             def transposes(b, m):
-                pts[(b, m)] = ps_t.tile([P, 4, P], F32, name="pt", tag="pt")
-                for u in range(4):
-                    nc.tensor.transpose(pts[(b, m)][:, u, :], xd[b][:, m, u, :].bitcast(F32), ident[:])
+                pts[(b, m)] = ps_t.tile([P, 8, P], BF16, name="pt", tag="pt")
+                for u in range(8):
+                    src = xs[b][:, u, :].rearrange("p (d m) -> p d m", m=3)
+                    nc.tensor.transpose(pts[(b, m)][:, u, :], src[:, :, m], ident[:])
 
             def copy_out(b, m):
                 if m == 0:
                     xg[b] = gpool.tile([P, 3, 4 * BT], BF16, name="xg", tag="xg", align_bytes=64)
-                dst = xg[b][:, m, :].bitcast(F32)
+                dst = xg[b][:, m, :]
                 src = pts[(b, m)][:].rearrange("p u c -> p (u c)")
-                if (b, m) in V_COPIES:
+                if m in V_COPY_M:
                     nc.vector.tensor_copy(out=dst, in_=src)
                 else:
                     nc.scalar.copy(out=dst, in_=src)
@@ -156,10 +149,7 @@ def tile_feedforwardse3_pa_t_kernel(tc, x, w_in, scale, bias, w_out, out):
 
             wr_in = wpool.tile([P, 4, 512], BF16, name="wr_in")
             wg_in = wpool.tile([P, 512, 4], BF16, name="wg_in", align_bytes=64)
-            nc.scalar.dma_start(
-                out=wr_in[:].rearrange("p (h e) f -> p h (e f)", h=2),
-                in_=w_in.rearrange("(h a e) f -> a h (e f)", h=2, e=2),
-            )
+            nc.scalar.dma_start(out=wr_in[:], in_=w_in.rearrange("(j p) f -> p j f", p=P))
             load_block(0)
             nc.scalar.dma_start(out=sc_raw[:], in_=scale.rearrange("a b (p j) -> (a b p) j", j=4))
             nc.scalar.dma_start(out=bi_raw[:], in_=bias.rearrange("a b (p j) -> (a b p) j", j=4))
@@ -181,28 +171,30 @@ def tile_feedforwardse3_pa_t_kernel(tc, x, w_in, scale, bias, w_out, out):
                     n = 6 * s + i
                     if i == 0 and ok(s - 1):
                         add2(s - 1)
+                    if i == 0 and ok(s + 1):
+                        copy_out(s + 1, 0)
                     if i == 0 and ok(s - 2) and s - 2 < NB - 2:
                         norm(s - 2)
-                    if 1 <= i <= 3 and ok(s + 1):
+                    if s + 1 == 0 and i == 0:
+                        quantise(wq_in[:], ws_in[:], wg_in[:].rearrange("p c j -> p (c j)"))
+                    if 1 <= i <= 2 and ok(s + 1):
                         quantise_x(s + 1, i - 1)
-                    if 1 <= i <= 3 and ok(s + 2):
-                        deinterleave(s + 2, i - 1)
-                        if s + 2 == 0 and i == 2:
-                            quantise(wq_in[:], ws_in[:], wg_in[:].rearrange("p c j -> p (c j)"))
-                        if i == 3 and s + 2 + XS_BUFS < NB:
-                            load_block(s + 2 + XS_BUFS)
-                        if i == 3 and s + 2 == NB - 1:
-                            nc.sync.dma_start(out=wr_out[:], in_=w_out.rearrange("(p j) d -> p j d", j=4))
                     if i == 4 and ok(s):
                         add1(s)
+                    if i == 4 and ok(s + 1):
+                        quantise_x(s + 1, 2)
                     if 0 <= n < 6 * NB:
                         square(n)
                     if 0 <= n + LA < 6 * NB:
                         stage1a(n + LA)
-                    if i < 3 and ok(s + 1):
+                    if 1 <= i <= 2 and ok(s + 1):
                         copy_out(s + 1, i)
                     if 1 <= i <= 3 and ok(s + 2):
                         transposes(s + 2, i - 1)
+                        if i == 3 and s + 2 + XS_BUFS < NB:
+                            load_block(s + 2 + XS_BUFS)
+                        if i == 3 and s + 2 == NB - 1:
+                            nc.sync.dma_start(out=wr_out[:], in_=w_out.rearrange("(p j) d -> p j d", j=4))
                     if i == 3 and ok(s - 1) and s - 1 < NB - 2:
                         rsqrt(s - 1)
             rsqrt(NB - 2)

@@ -14,280 +14,318 @@ ACT = mybir.ActivationFunctionType
 ALU = mybir.AluOpType
 
 P = 128
-NCH = 16
-NB = 8
-BT = 256
-E = 1536
-TOK = 2048
-LA = 5
-V_COPY_M = (0, 2)
-V_OUT = ((15, 1), (15, 3))
-XS_BUFS = 4
-RN_MAX = 1.0e12
+TOKENS = 2048
+ROW = 1536
+CHUNK = 128
+GROUP = 256
+N_CHUNKS = TOKENS // CHUNK
+N_GROUPS = TOKENS // GROUP
+STEPS = 6
+H_BANKS = 5
+X_TILES = 4
+MAX_INV_NORM = 1.0e12
+VECTOR_COPIES_M = (0, 2)
 
 
 def tile_feedforwardse3_pa_t_kernel(tc, x, w_in, scale, bias, w_out, out):
     nc = tc.nc
-    xv = x.rearrange("b n (j d) m -> (b n j) (d m)", j=4).rearrange("(u p) e -> p u e", p=P)
-    ov = out.rearrange("b n d m -> (b n) (d m)").rearrange("(c p) e -> p c e", p=P)
+    x_units = x.rearrange("b n (j d) m -> (b n j) (d m)", j=4).rearrange("(u p) e -> p u e", p=P)
+    out_chunks = out.rearrange("b n d m -> (b n) (d m)").rearrange("(c p) e -> p c e", p=P)
 
     with ExitStack() as ctx:
         ctx.enter_context(tc.manual_schedule())
         keep = ctx.enter_context(tc.tile_pool(name="keep", bufs=1))
 
-        ident = keep.tile([P, P], BF16, name="ident")
-        wq_in = keep.tile([P, 512], U32, name="wq_in", align_bytes=64)
-        ws_in = keep.tile([P, 512], U8, name="ws_in", align_bytes=64)
-        wq_out = keep.tile([P, 512], U32, name="wq_out", align_bytes=64)
-        ws_out = keep.tile([P, 512], U8, name="ws_out", align_bytes=64)
-        wr_out = keep.tile([P, 4, 512], BF16, name="wr_out")
-        wg_out = keep.tile([P, 512, 4], BF16, name="wg_out", align_bytes=64)
-        xq = keep.tile([P, 3, TOK], U32, name="xq", align_bytes=64)
-        xsc = keep.tile([P, 3, TOK], U8, name="xsc", align_bytes=64)
-        a1 = keep.tile([P, 4, TOK], F32, name="a1")
-        a2 = keep.tile([P, 4, TOK], F32, name="a2")
-        sc_raw = keep.tile([P, 4], BF16, name="sc_raw")
-        bi_raw = keep.tile([P, 4], BF16, name="bi_raw")
-        sc = keep.tile([P, 4], F32, name="sc")
-        bi = keep.tile([P, 4], F32, name="bi")
+        identity = keep.tile([P, P], BF16, name="identity")
+        w_in_words = keep.tile([P, 512], U32, name="w_in_words", align_bytes=64)
+        w_in_scales = keep.tile([P, 512], U8, name="w_in_scales", align_bytes=64)
+        w_out_words = keep.tile([P, 512], U32, name="w_out_words", align_bytes=64)
+        w_out_scales = keep.tile([P, 512], U8, name="w_out_scales", align_bytes=64)
+        x_words = keep.tile([P, 3, TOKENS], U32, name="x_words", align_bytes=64)
+        x_scales = keep.tile([P, 3, TOKENS], U8, name="x_scales", align_bytes=64)
+        w_out_rows = keep.tile([P, 4, 512], BF16, name="w_out_rows")
+        w_out_grouped = keep.tile([P, 512, 4], BF16, name="w_out_grouped", align_bytes=64)
+        norms = keep.tile([P, 4, TOKENS], F32, name="norms")
+        factors = keep.tile([P, 4, TOKENS], F32, name="factors")
+        scale_bf = keep.tile([P, 4], BF16, name="scale_bf")
+        bias_bf = keep.tile([P, 4], BF16, name="bias_bf")
+        scale_f32 = keep.tile([P, 4], F32, name="scale_f32")
+        bias_f32 = keep.tile([P, 4], F32, name="bias_f32")
         one = keep.tile([P, 1], F32, name="one")
-        one2 = keep.tile([P, 1], F32, name="one2")
+        unused = keep.tile([P, 1], F32, name="unused")
 
-        def quantise(codes, scales, src):
-            nc.vector.quantize_mx(out=codes.bitcast(FP8X4), scales=scales, in_=src)
+        def quantise(words, scales, values):
+            nc.vector.quantize_mx(out=words.bitcast(FP8X4), scales=scales, in_=values)
 
-        def mx(dst, lw, ls, rw, rs):
+        def matmul_mx(acc, lhs_words, lhs_scales, rhs_words, rhs_scales):
             nc.tensor.matmul_mx(
-                out=dst,
-                lhsT=lw.bitcast(FP8X4),
-                lhsT_scale=ls,
-                rhs=rw.bitcast(FP8X4),
-                rhs_scale=rs,
+                out=acc,
+                lhsT=lhs_words.bitcast(FP8X4),
+                lhsT_scale=lhs_scales,
+                rhs=rhs_words.bitcast(FP8X4),
+                rhs_scale=rhs_scales,
                 start=True,
                 stop=True,
             )
 
-        with ExitStack() as actx:
-            xpool = actx.enter_context(tc.tile_pool(name="xpool", bufs=XS_BUFS))
-            gpool = actx.enter_context(tc.tile_pool(name="gpool", bufs=3))
-            qpool = actx.enter_context(tc.tile_pool(name="qpool", bufs=3))
-            wpool = actx.enter_context(tc.tile_pool(name="wpool", bufs=1))
-            ps_t = actx.enter_context(tc.psum_pool(name="ps_t", bufs=3))
-            ps_h = actx.enter_context(tc.psum_pool(name="ps_h", bufs=LA))
+        def hidden(j):
+            return slice(P * j, P * (j + 1))
 
-            xs = {}
-            xg = {}
-            sq = {}
-            pts = {}
-            hh = {}
+        with ExitStack() as part1:
+            x_pool = part1.enter_context(tc.tile_pool(name="x_pool", bufs=X_TILES))
+            grouped_pool = part1.enter_context(tc.tile_pool(name="grouped_pool", bufs=3))
+            square_pool = part1.enter_context(tc.tile_pool(name="square_pool", bufs=3))
+            w_pool = part1.enter_context(tc.tile_pool(name="w_pool", bufs=1))
+            xt_psum = part1.enter_context(tc.psum_pool(name="xt_psum", bufs=3))
+            h_psum = part1.enter_context(tc.psum_pool(name="h_psum", bufs=H_BANKS))
 
-            def ok(b):
-                return 0 <= b < NB
+            x_rows = {}
+            x_transposed = {}
+            x_grouped = {}
+            h_banks = {}
+            squares = {}
 
-            def load_block(b):
-                xs[b] = xpool.tile([P, 8, 384], BF16, name="xs", tag="xs")
-                nc.sync.dma_start(out=xs[b][:], in_=xv[:, 8 * b : 8 * b + 8, :])
+            def is_group(g):
+                return 0 <= g < N_GROUPS
 
-            def transposes(b, m):
-                pts[(b, m)] = ps_t.tile([P, 8, P], BF16, name="pt", tag="pt")
+            def tokens_of(g):
+                return slice(GROUP * g, GROUP * (g + 1))
+
+            def load_x(g):
+                x_rows[g] = x_pool.tile([P, 8, 384], BF16, name="x_rows", tag="x_rows")
+                nc.sync.dma_start(out=x_rows[g][:], in_=x_units[:, 8 * g : 8 * g + 8, :])
+
+            def transpose_x(g, m):
+                x_transposed[(g, m)] = xt_psum.tile([P, 8, P], BF16, name="x_transposed", tag="x_transposed")
                 for u in range(8):
-                    src = xs[b][:, u, :].rearrange("p (d m) -> p d m", m=3)
-                    nc.tensor.transpose(pts[(b, m)][:, u, :], src[:, :, m], ident[:])
+                    columns = x_rows[g][:, u, :].rearrange("p (d m) -> p d m", m=3)
+                    nc.tensor.transpose(x_transposed[(g, m)][:, u, :], columns[:, :, m], identity[:])
 
-            def copy_out(b, m):
+            def copy_x(g, m):
                 if m == 0:
-                    xg[b] = gpool.tile([P, 3, 4 * BT], BF16, name="xg", tag="xg", align_bytes=64)
-                dst = xg[b][:, m, :]
-                src = pts[(b, m)][:].rearrange("p u c -> p (u c)")
-                if m in V_COPY_M:
-                    nc.vector.tensor_copy(out=dst, in_=src)
+                    x_grouped[g] = grouped_pool.tile(
+                        [P, 3, 4 * GROUP], BF16, name="x_grouped", tag="x_grouped", align_bytes=64
+                    )
+                bank = x_transposed[(g, m)][:].rearrange("p u c -> p (u c)")
+                if m in VECTOR_COPIES_M:
+                    nc.vector.tensor_copy(out=x_grouped[g][:, m, :], in_=bank)
                 else:
-                    nc.scalar.copy(out=dst, in_=src)
+                    nc.scalar.copy(out=x_grouped[g][:, m, :], in_=bank)
 
-            def quantise_x(b, m):
-                cols = slice(BT * b, BT * (b + 1))
-                quantise(xq[:, m, cols], xsc[:, m, cols], xg[b][:, m, :])
+            def quantise_x(g, m):
+                quantise(x_words[:, m, tokens_of(g)], x_scales[:, m, tokens_of(g)], x_grouped[g][:, m, :])
 
-            def stage1a(n):
-                b, i = divmod(n, 6)
-                m, jp = divmod(i, 2)
-                cols = slice(BT * b, BT * (b + 1))
-                hh[n] = ps_h.tile([P, 2, BT], F32, name="hh", tag="hh")
-                for jj in range(2):
-                    j = 2 * jp + jj
-                    mx(
-                        hh[n][:, jj, :],
-                        wq_in[:, P * j : P * (j + 1)],
-                        ws_in[:, P * j : P * (j + 1)],
-                        xq[:, m, cols],
-                        xsc[:, m, cols],
+            def first_matmul(bank):
+                g, step = divmod(bank, STEPS)
+                m, half = divmod(step, 2)
+                h_banks[bank] = h_psum.tile([P, 2, GROUP], F32, name="h_bank", tag="h_bank")
+                for i in range(2):
+                    j = 2 * half + i
+                    matmul_mx(
+                        h_banks[bank][:, i, :],
+                        w_in_words[:, hidden(j)],
+                        w_in_scales[:, hidden(j)],
+                        x_words[:, m, tokens_of(g)],
+                        x_scales[:, m, tokens_of(g)],
                     )
 
-            def square(n):
-                b, i = divmod(n, 6)
-                m, jp = divmod(i, 2)
-                if i == 0:
-                    sq[b] = qpool.tile([P, 3, 4, BT], F32, name="sq", tag="sq")
-                nc.scalar.activation(out=sq[b][:, m, 2 * jp : 2 * jp + 2, :], in_=hh[n][:], func=ACT.Square)
-
-            def add1(b):
-                nc.vector.tensor_tensor(out=sq[b][:, 0, :, :], in0=sq[b][:, 0, :, :], in1=sq[b][:, 1, :, :], op=ALU.add)
-
-            def add2(b):
-                cols = slice(BT * b, BT * (b + 1))
-                nc.vector.tensor_tensor(out=a1[:, :, cols], in0=sq[b][:, 0, :, :], in1=sq[b][:, 2, :, :], op=ALU.add)
-
-            def rsqrt(b):
-                cols = slice(BT * b, BT * (b + 1))
-                nc.scalar.activation(out=a2[:, :, cols], in_=a1[:, :, cols], func=ACT.Abs_reciprocal_sqrt)
-
-            def norm(b):
-                cols = slice(BT * b, BT * (b + 1))
-                nc.vector.scalar_tensor_tensor(
-                    out=a1[:, :, cols], in0=a2[:, :, cols], scalar=RN_MAX, in1=a1[:, :, cols], op0=ALU.min, op1=ALU.mult
-                )
-
-            wr_in = wpool.tile([P, 4, 512], BF16, name="wr_in")
-            wg_in = wpool.tile([P, 512, 4], BF16, name="wg_in", align_bytes=64)
-            nc.scalar.dma_start(out=wr_in[:], in_=w_in.rearrange("(j p) f -> p j f", p=P))
-            load_block(0)
-            nc.scalar.dma_start(out=sc_raw[:], in_=scale.rearrange("a b (p j) -> (a b p) j", j=4))
-            nc.scalar.dma_start(out=bi_raw[:], in_=bias.rearrange("a b (p j) -> (a b p) j", j=4))
-            make_identity(nc, ident[:])
-            nc.vector.memset(one[:], 1.0)
-            nc.scalar.activation(out=one2[:], in_=one[:], func=ACT.Abs_reciprocal_sqrt)
-            for b in range(1, XS_BUFS):
-                load_block(b)
-
-            wsrc = wr_in[:].rearrange("p j (b a) -> p a b j", a=4)
-            wdst = wg_in[:].rearrange("p (a b) j -> p a b j", a=4)
-            nc.vector.tensor_copy(out=wdst[:, 0:2, :, :], in_=wsrc[:, 0:2, :, :])
-            nc.scalar.copy(out=wdst[:, 2:4, :, :], in_=wsrc[:, 2:4, :, :])
-            nc.scalar.copy(out=sc[:], in_=sc_raw[:])
-            nc.scalar.copy(out=bi[:], in_=bi_raw[:])
-
-            for s in range(-2, NB + 2):
-                for i in range(6):
-                    n = 6 * s + i
-                    if i == 0 and ok(s - 1):
-                        add2(s - 1)
-                    if i == 0 and ok(s + 1):
-                        copy_out(s + 1, 0)
-                    if i == 0 and ok(s - 2) and s - 2 < NB - 2:
-                        norm(s - 2)
-                    if s + 1 == 0 and i == 0:
-                        quantise(wq_in[:], ws_in[:], wg_in[:].rearrange("p c j -> p (c j)"))
-                    if 1 <= i <= 2 and ok(s + 1):
-                        quantise_x(s + 1, i - 1)
-                    if i == 4 and ok(s):
-                        add1(s)
-                    if i == 4 and ok(s + 1):
-                        quantise_x(s + 1, 2)
-                    if 0 <= n < 6 * NB:
-                        square(n)
-                    if 0 <= n + LA < 6 * NB:
-                        stage1a(n + LA)
-                    if 1 <= i <= 2 and ok(s + 1):
-                        copy_out(s + 1, i)
-                    if 1 <= i <= 3 and ok(s + 2):
-                        transposes(s + 2, i - 1)
-                        if i == 3 and s + 2 + XS_BUFS < NB:
-                            load_block(s + 2 + XS_BUFS)
-                        if i == 3 and s + 2 == NB - 1:
-                            nc.sync.dma_start(out=wr_out[:], in_=w_out.rearrange("(p j) d -> p j d", j=4))
-                    if i == 3 and ok(s - 1) and s - 1 < NB - 2:
-                        rsqrt(s - 1)
-            rsqrt(NB - 2)
-            norm(NB - 2)
-            rsqrt(NB - 1)
-            nc.vector.tensor_copy(out=wg_out[:], in_=wr_out[:].rearrange("p j d -> p d j"))
-            norm(NB - 1)
-            quantise(wq_out[:], ws_out[:], wg_out[:].rearrange("p c j -> p (c j)"))
-
-        with ExitStack() as bctx:
-            hpool = bctx.enter_context(tc.tile_pool(name="hpool", bufs=3))
-            opool = bctx.enter_context(tc.tile_pool(name="opool", bufs=6))
-            ps_b = bctx.enter_context(tc.psum_pool(name="ps_b", bufs=4))
-            ps_o = bctx.enter_context(tc.psum_pool(name="ps_o", bufs=4))
-
-            def gelu(t0, w, j):
+            def square(bank):
+                g, step = divmod(bank, STEPS)
+                m, half = divmod(step, 2)
+                if step == 0:
+                    squares[g] = square_pool.tile([P, 3, 4, GROUP], F32, name="squares", tag="squares")
                 nc.scalar.activation(
-                    out=a1[:, j, t0 : t0 + w],
-                    in_=a1[:, j, t0 : t0 + w],
-                    func=ACT.Gelu,
-                    bias=bi[:, j : j + 1],
-                    scale=sc[:, j : j + 1],
+                    out=squares[g][:, m, 2 * half : 2 * half + 2, :], in_=h_banks[bank][:], func=ACT.Square
                 )
 
-            def factor(t0, w):
-                cols = slice(t0, t0 + w)
+            def add_first_two(g):
+                nc.vector.tensor_tensor(
+                    out=squares[g][:, 0, :, :], in0=squares[g][:, 0, :, :], in1=squares[g][:, 1, :, :], op=ALU.add
+                )
+
+            def add_third(g):
+                nc.vector.tensor_tensor(
+                    out=norms[:, :, tokens_of(g)], in0=squares[g][:, 0, :, :], in1=squares[g][:, 2, :, :], op=ALU.add
+                )
+
+            def inverse_root(g):
+                nc.scalar.activation(
+                    out=factors[:, :, tokens_of(g)], in_=norms[:, :, tokens_of(g)], func=ACT.Abs_reciprocal_sqrt
+                )
+
+            def norm(g):
                 nc.vector.scalar_tensor_tensor(
-                    out=a2[:, :, cols], in0=a2[:, :, cols], scalar=RN_MAX, in1=a1[:, :, cols], op0=ALU.min, op1=ALU.mult
+                    out=norms[:, :, tokens_of(g)],
+                    in0=factors[:, :, tokens_of(g)],
+                    scalar=MAX_INV_NORM,
+                    in1=norms[:, :, tokens_of(g)],
+                    op0=ALU.min,
+                    op1=ALU.mult,
                 )
 
-            hbs = {}
+            w_in_rows = w_pool.tile([P, 4, 512], BF16, name="w_in_rows")
+            w_in_grouped = w_pool.tile([P, 512, 4], BF16, name="w_in_grouped", align_bytes=64)
+            load_x(0)
+            nc.sync.dma_start(out=w_in_rows[:], in_=w_in.rearrange("(j p) f -> p j f", p=P))
+            nc.scalar.dma_start(out=scale_bf[:], in_=scale.rearrange("a b (p j) -> (a b p) j", j=4))
+            nc.scalar.dma_start(out=bias_bf[:], in_=bias.rearrange("a b (p j) -> (a b p) j", j=4))
+            make_identity(nc, identity[:])
+            nc.vector.memset(one[:], 1.0)
+            nc.scalar.activation(out=unused[:], in_=one[:], func=ACT.Abs_reciprocal_sqrt)
+            for g in range(1, X_TILES):
+                load_x(g)
 
-            def stage1b(c, m):
-                hb = ps_b.tile([P, 4, P], F32, name="hb", tag="hb")
-                hbs[(c, m)] = hb
+            sorted_rows = w_in_rows[:].rearrange("p j (b a) -> p a b j", a=4)
+            sorted_grouped = w_in_grouped[:].rearrange("p (a b) j -> p a b j", a=4)
+            nc.vector.tensor_copy(out=sorted_grouped[:, 0:2, :, :], in_=sorted_rows[:, 0:2, :, :])
+            nc.scalar.copy(out=sorted_grouped[:, 2:4, :, :], in_=sorted_rows[:, 2:4, :, :])
+            nc.scalar.copy(out=scale_f32[:], in_=scale_bf[:])
+            nc.scalar.copy(out=bias_f32[:], in_=bias_bf[:])
+
+            for g in range(-2, N_GROUPS + 1):
+                for step in range(STEPS):
+                    bank = STEPS * g + step
+                    if step == 0 and is_group(g - 1):
+                        add_third(g - 1)
+                    if step == 0 and is_group(g + 1):
+                        copy_x(g + 1, 0)
+                    if step == 0 and is_group(g - 2) and g - 2 < N_GROUPS - 2:
+                        norm(g - 2)
+                    if step == 0 and g + 1 == 0:
+                        quantise(w_in_words[:], w_in_scales[:], w_in_grouped[:].rearrange("p c j -> p (c j)"))
+                    if step in (1, 2) and is_group(g + 1):
+                        quantise_x(g + 1, step - 1)
+                    if step == 4 and is_group(g):
+                        add_first_two(g)
+                    if step == 4 and is_group(g + 1):
+                        quantise_x(g + 1, 2)
+                    if is_group(g):
+                        square(bank)
+                    if 0 <= bank + H_BANKS < STEPS * N_GROUPS:
+                        first_matmul(bank + H_BANKS)
+                    if step in (1, 2) and is_group(g + 1):
+                        copy_x(g + 1, step)
+                    if step == 2 and is_group(g + 2):
+                        transpose_x(g + 2, 0)
+                        transpose_x(g + 2, 1)
+                    if step == 4 and is_group(g + 2):
+                        transpose_x(g + 2, 2)
+                        if g + 2 + X_TILES < N_GROUPS:
+                            load_x(g + 2 + X_TILES)
+                        if g + 2 == N_GROUPS - 1:
+                            nc.sync.dma_start(out=w_out_rows[:], in_=w_out.rearrange("(p j) d -> p j d", j=4))
+                    if step == 3 and is_group(g - 1) and g - 1 < N_GROUPS - 2:
+                        inverse_root(g - 1)
+            inverse_root(N_GROUPS - 2)
+            norm(N_GROUPS - 2)
+            inverse_root(N_GROUPS - 1)
+            nc.vector.tensor_copy(out=w_out_grouped[:], in_=w_out_rows[:].rearrange("p j d -> p d j"))
+            norm(N_GROUPS - 1)
+            quantise(w_out_words[:], w_out_scales[:], w_out_grouped[:].rearrange("p c j -> p (c j)"))
+
+        with ExitStack() as part2:
+            g_pool = part2.enter_context(tc.tile_pool(name="g_pool", bufs=3))
+            out_pool = part2.enter_context(tc.tile_pool(name="out_pool", bufs=6))
+            h_again_psum = part2.enter_context(tc.psum_pool(name="h_again_psum", bufs=4))
+            out_psum = part2.enter_context(tc.psum_pool(name="out_psum", bufs=4))
+
+            h_again = {}
+
+            def gelu(first, count, j):
+                nc.scalar.activation(
+                    out=norms[:, j, first : first + count],
+                    in_=norms[:, j, first : first + count],
+                    func=ACT.Gelu,
+                    bias=bias_f32[:, j : j + 1],
+                    scale=scale_f32[:, j : j + 1],
+                )
+
+            def factor(first, count):
+                span = slice(first, first + count)
+                nc.vector.scalar_tensor_tensor(
+                    out=factors[:, :, span],
+                    in0=factors[:, :, span],
+                    scalar=MAX_INV_NORM,
+                    in1=norms[:, :, span],
+                    op0=ALU.min,
+                    op1=ALU.mult,
+                )
+
+            def first_matmul_again(c, m):
+                tokens = slice(CHUNK * c, CHUNK * (c + 1))
+                h_again[(c, m)] = h_again_psum.tile([P, 4, CHUNK], F32, name="h_again", tag="h_again")
                 for j in range(4):
-                    mx(
-                        hb[:, j, :],
-                        wq_in[:, P * j : P * (j + 1)],
-                        ws_in[:, P * j : P * (j + 1)],
-                        xq[:, m, P * c : P * (c + 1)],
-                        xsc[:, m, P * c : P * (c + 1)],
+                    matmul_mx(
+                        h_again[(c, m)][:, j, :],
+                        w_in_words[:, hidden(j)],
+                        w_in_scales[:, hidden(j)],
+                        x_words[:, m, tokens],
+                        x_scales[:, m, tokens],
                     )
 
-            late = [(t0, j) for t0 in (1024, 1536) for j in range(4)]
             for m in range(3):
-                stage1b(0, m)
-            for t0, w in ((0, 128), (128, 128), (256, 256), (512, 512)):
+                first_matmul_again(0, m)
+            for first, count in ((0, 128), (128, 128), (256, 256), (512, 512)):
                 for j in range(4):
-                    gelu(t0, w, j)
-                if t0 == 0:
-                    factor(0, 128)
-            for c in range(NCH):
-                if c + 1 < NCH:
-                    stage1b(c + 1, 0)
-                gg = hpool.tile([P, 3, P, 4], BF16, name="gg", tag="gg", align_bytes=64)
-                gq = hpool.tile([P, 3 * P], U32, name="gq", tag="gq", align_bytes=64)
-                gs = hpool.tile([P, 3 * P], U8, name="gs", tag="gs", align_bytes=64)
-                fac = a2[:, :, P * c : P * (c + 1)].rearrange("p j t -> p t j")
+                    gelu(first, count, j)
+                if first == 0:
+                    factor(0, CHUNK)
+            later_gelus = [(first, j) for first in (1024, 1536) for j in range(4)]
+
+            for c in range(N_CHUNKS):
+                last = c == N_CHUNKS - 1
+                if not last:
+                    first_matmul_again(c + 1, 0)
+                g_grouped = g_pool.tile([P, 3, CHUNK, 4], BF16, name="g_grouped", tag="g_grouped", align_bytes=64)
+                g_words = g_pool.tile([P, 3 * CHUNK], U32, name="g_words", tag="g_words", align_bytes=64)
+                g_scales = g_pool.tile([P, 3 * CHUNK], U8, name="g_scales", tag="g_scales", align_bytes=64)
+                chunk_factors = factors[:, :, CHUNK * c : CHUNK * (c + 1)].rearrange("p j t -> p t j")
                 for m in range(3):
                     nc.vector.tensor_tensor(
-                        out=gg[:, m, :, :], in0=hbs[(c, m)][:].rearrange("p j t -> p t j"), in1=fac, op=ALU.mult
+                        out=g_grouped[:, m, :, :],
+                        in0=h_again[(c, m)][:].rearrange("p j t -> p t j"),
+                        in1=chunk_factors,
+                        op=ALU.mult,
                     )
-                    if m < 2 and c + 1 < NCH:
-                        stage1b(c + 1, m + 1)
-                quantise(gq[:, 0 : 2 * P], gs[:, 0 : 2 * P], gg[:, 0:2, :, :].rearrange("p m t j -> p (m t j)"))
-                quantise(gq[:, 2 * P : 3 * P], gs[:, 2 * P : 3 * P], gg[:, 2, :, :].rearrange("p t j -> p (t j)"))
+                    if m < 2 and not last:
+                        first_matmul_again(c + 1, m + 1)
+                quantise(
+                    g_words[:, 0 : 2 * CHUNK],
+                    g_scales[:, 0 : 2 * CHUNK],
+                    g_grouped[:, 0:2, :, :].rearrange("p m t j -> p (m t j)"),
+                )
+                quantise(
+                    g_words[:, 2 * CHUNK : 3 * CHUNK],
+                    g_scales[:, 2 * CHUNK : 3 * CHUNK],
+                    g_grouped[:, 2, :, :].rearrange("p t j -> p (t j)"),
+                )
                 if c == 0:
-                    factor(128, 128)
-                if c % 2 == 0 and c // 2 + 1 < NB:
-                    factor(BT * (c // 2 + 1), BT)
-                ot = opool.tile([P, E], F32, name="ot", tag="ot")
-                for dq in range(4):
-                    ob = ps_o.tile([P, 3, P], F32, name="ob", tag="ob")
+                    factor(CHUNK, CHUNK)
+                if c % 2 == 0 and c + 2 < N_CHUNKS:
+                    factor(CHUNK * (c + 2), 2 * CHUNK)
+
+                out_rows = out_pool.tile([P, ROW], F32, name="out_rows", tag="out_rows")
+                for quarter in range(4):
+                    channels = slice(P * quarter, P * (quarter + 1))
+                    acc = out_psum.tile([P, 3, P], F32, name="acc", tag="acc")
                     for m in range(3):
-                        mx(
-                            ob[:, m, :],
-                            gq[:, P * m : P * (m + 1)],
-                            gs[:, P * m : P * (m + 1)],
-                            wq_out[:, P * dq : P * (dq + 1)],
-                            ws_out[:, P * dq : P * (dq + 1)],
+                        matmul_mx(
+                            acc[:, m, :],
+                            g_words[:, CHUNK * m : CHUNK * (m + 1)],
+                            g_scales[:, CHUNK * m : CHUNK * (m + 1)],
+                            w_out_words[:, channels],
+                            w_out_scales[:, channels],
                         )
-                    dst = ot[:, 384 * dq : 384 * (dq + 1)].rearrange("p (d m) -> p d m", m=3)
-                    src = ob[:].rearrange("p m d -> p d m")
-                    if (c, dq) in V_OUT:
-                        nc.vector.tensor_copy(out=dst, in_=src)
+                    interleaved = out_rows[:, 384 * quarter : 384 * (quarter + 1)].rearrange("p (d m) -> p d m", m=3)
+                    if last and quarter % 2 == 1:
+                        nc.vector.tensor_copy(out=interleaved, in_=acc[:].rearrange("p m d -> p d m"))
                     else:
-                        nc.scalar.copy(out=dst, in_=src)
-                    if c == NCH - 1 and dq == 1:
-                        nc.sync.dma_start(out=ov[:, c, 0:768], in_=ot[:, 0:768])
-                if c == NCH - 1:
-                    nc.sync.dma_start(out=ov[:, c, 768:E], in_=ot[:, 768:E])
+                        nc.scalar.copy(out=interleaved, in_=acc[:].rearrange("p m d -> p d m"))
+                    if last and quarter == 1:
+                        nc.sync.dma_start(out=out_chunks[:, c, 0 : ROW // 2], in_=out_rows[:, 0 : ROW // 2])
+                if last:
+                    nc.sync.dma_start(out=out_chunks[:, c, ROW // 2 : ROW], in_=out_rows[:, ROW // 2 : ROW])
                 else:
-                    nc.sync.dma_start(out=ov[:, c, :], in_=ot[:])
-                if c < len(late):
-                    gelu(late[c][0], 512, late[c][1])
+                    nc.sync.dma_start(out=out_chunks[:, c, :], in_=out_rows[:])
+                if c < len(later_gelus):
+                    gelu(later_gelus[c][0], 512, later_gelus[c][1])

@@ -225,11 +225,13 @@ def tile_feedforwardse3_pa_t_kernel(tc, x, w_in, scale, bias, w_out, out):
 
         with ExitStack() as part2:
             g_pool = part2.enter_context(tc.tile_pool(name="g_pool", bufs=3))
+            factor_pool = part2.enter_context(tc.tile_pool(name="factor_pool", bufs=4))
             out_pool = part2.enter_context(tc.tile_pool(name="out_pool", bufs=6))
             h_again_psum = part2.enter_context(tc.psum_pool(name="h_again_psum", bufs=4))
             out_psum = part2.enter_context(tc.psum_pool(name="out_psum", bufs=4))
 
             h_again = {}
+            chunk_factors = {}
 
             def gelu(first, count, j):
                 nc.scalar.activation(
@@ -242,14 +244,17 @@ def tile_feedforwardse3_pa_t_kernel(tc, x, w_in, scale, bias, w_out, out):
 
             def factor(first, count):
                 span = slice(first, first + count)
+                tile = factor_pool.tile([P, 2 * CHUNK, 4], F32, name="factor_tile", tag="factor_tile")
                 nc.vector.scalar_tensor_tensor(
-                    out=factors[:, :, span],
-                    in0=factors[:, :, span],
+                    out=tile[:, 0:count, :],
+                    in0=factors[:, :, span].rearrange("p j t -> p t j"),
                     scalar=MAX_INV_NORM,
-                    in1=norms[:, :, span],
+                    in1=norms[:, :, span].rearrange("p j t -> p t j"),
                     op0=ALU.min,
                     op1=ALU.mult,
                 )
+                for k in range(count // CHUNK):
+                    chunk_factors[first // CHUNK + k] = tile[:, CHUNK * k : CHUNK * (k + 1), :]
 
             def first_matmul_again(c, m):
                 tokens = slice(CHUNK * c, CHUNK * (c + 1))
@@ -279,12 +284,11 @@ def tile_feedforwardse3_pa_t_kernel(tc, x, w_in, scale, bias, w_out, out):
                 g_grouped = g_pool.tile([P, 3, CHUNK, 4], BF16, name="g_grouped", tag="g_grouped", align_bytes=64)
                 g_words = g_pool.tile([P, 3 * CHUNK], U32, name="g_words", tag="g_words", align_bytes=64)
                 g_scales = g_pool.tile([P, 3 * CHUNK], U8, name="g_scales", tag="g_scales", align_bytes=64)
-                chunk_factors = factors[:, :, CHUNK * c : CHUNK * (c + 1)].rearrange("p j t -> p t j")
                 for m in range(3):
                     nc.vector.tensor_tensor(
                         out=g_grouped[:, m, :, :],
                         in0=h_again[(c, m)][:].rearrange("p j t -> p t j"),
-                        in1=chunk_factors,
+                        in1=chunk_factors[c],
                         op=ALU.mult,
                     )
                     if m < 2 and not last:

@@ -20,8 +20,7 @@ CHUNK = 128
 GROUP = 256
 N_CHUNKS = TOKENS // CHUNK
 N_GROUPS = TOKENS // GROUP
-STEPS = 6
-H_BANKS = 5
+UNITS = 4
 X_TILES = 4
 MAX_INV_NORM = 1.0e12
 VECTOR_COPIES_M = (0, 2)
@@ -29,14 +28,14 @@ VECTOR_COPIES_M = (0, 2)
 
 def tile_feedforwardse3_pa_t_kernel(tc, x, w_in, scale, bias, w_out, out):
     nc = tc.nc
-    x_units = x.rearrange("b n (j d) m -> (b n j) (d m)", j=4).rearrange("(u p) e -> p u e", p=P)
+    x_units = x.rearrange("b n (h d) m -> (b n h) (d m)", h=2).rearrange("(u p) e -> p u e", p=P)
     out_chunks = out.rearrange("b n d m -> (b n) (d m)").rearrange("(c p) e -> p c e", p=P)
 
     with ExitStack() as ctx:
         ctx.enter_context(tc.manual_schedule())
         keep = ctx.enter_context(tc.tile_pool(name="keep", bufs=1))
 
-        identity = keep.tile([P, P], BF16, name="identity")
+        identity = keep.tile([P, P], F32, name="identity")
         w_in_words = keep.tile([P, 512], U32, name="w_in_words", align_bytes=64)
         w_in_scales = keep.tile([P, 512], U8, name="w_in_scales", align_bytes=64)
         w_out_words = keep.tile([P, 512], U32, name="w_out_words", align_bytes=64)
@@ -73,92 +72,102 @@ def tile_feedforwardse3_pa_t_kernel(tc, x, w_in, scale, bias, w_out, out):
 
         with ExitStack() as part1:
             x_pool = part1.enter_context(tc.tile_pool(name="x_pool", bufs=X_TILES))
-            grouped_pool = part1.enter_context(tc.tile_pool(name="grouped_pool", bufs=3))
+            plane_pool = part1.enter_context(tc.tile_pool(name="plane_pool", bufs=2))
+            grouped_pool = part1.enter_context(tc.tile_pool(name="grouped_pool", bufs=2))
             square_pool = part1.enter_context(tc.tile_pool(name="square_pool", bufs=3))
             w_pool = part1.enter_context(tc.tile_pool(name="w_pool", bufs=1))
-            xt_psum = part1.enter_context(tc.psum_pool(name="xt_psum", bufs=3))
-            h_psum = part1.enter_context(tc.psum_pool(name="h_psum", bufs=H_BANKS))
+            xt_psum = part1.enter_context(tc.psum_pool(name="xt_psum", bufs=2))
+            h_psum = part1.enter_context(tc.psum_pool(name="h_psum", bufs=4))
+            sum_psum = part1.enter_context(tc.psum_pool(name="sum_psum", bufs=2))
 
             x_rows = {}
+            x_planes = {}
             x_transposed = {}
             x_grouped = {}
             h_banks = {}
             squares = {}
+            sums = {}
 
             def is_group(g):
                 return 0 <= g < N_GROUPS
 
-            def tokens_of(g):
+            def is_chunk(c):
+                return 0 <= c < N_CHUNKS
+
+            def tokens_of_group(g):
                 return slice(GROUP * g, GROUP * (g + 1))
 
+            def tokens_of_chunk(c):
+                return slice(CHUNK * c, CHUNK * (c + 1))
+
             def load_x(g):
-                x_rows[g] = x_pool.tile([P, 8, 384], BF16, name="x_rows", tag="x_rows")
-                nc.sync.dma_start(out=x_rows[g][:], in_=x_units[:, 8 * g : 8 * g + 8, :])
+                x_rows[g] = x_pool.tile([P, UNITS, 768], BF16, name="x_rows", tag="x_rows")
+                nc.sync.dma_start(out=x_rows[g][:], in_=x_units[:, UNITS * g : UNITS * (g + 1), :])
+
+            def part_x(g, m):
+                if m == 0:
+                    x_planes[g] = plane_pool.tile([P, 3, UNITS, 256], BF16, name="x_planes", tag="x_planes")
+                rows = x_rows[g][:].rearrange("p u (d m) -> p u d m", m=3)
+                nc.vector.tensor_copy(out=x_planes[g][:, m, :, :], in_=rows[:, :, :, m])
 
             def transpose_x(g, m):
-                x_transposed[(g, m)] = xt_psum.tile([P, 8, P], BF16, name="x_transposed", tag="x_transposed")
-                for u in range(8):
-                    columns = x_rows[g][:, u, :].rearrange("p (d m) -> p d m", m=3)
-                    nc.tensor.transpose(x_transposed[(g, m)][:, u, :], columns[:, :, m], identity[:])
+                x_transposed[(g, m)] = xt_psum.tile([P, UNITS, P], F32, name="x_transposed", tag="x_transposed")
+                for u in range(UNITS):
+                    words = x_planes[g][:, m, u, :].bitcast(F32)
+                    nc.tensor.transpose(x_transposed[(g, m)][:, u, :], words, identity[:])
 
             def copy_x(g, m):
                 if m == 0:
                     x_grouped[g] = grouped_pool.tile(
                         [P, 3, 4 * GROUP], BF16, name="x_grouped", tag="x_grouped", align_bytes=64
                     )
+                words = x_grouped[g][:, m, :].bitcast(F32)
                 bank = x_transposed[(g, m)][:].rearrange("p u c -> p (u c)")
                 if m in VECTOR_COPIES_M:
-                    nc.vector.tensor_copy(out=x_grouped[g][:, m, :], in_=bank)
+                    nc.vector.tensor_copy(out=words, in_=bank)
                 else:
-                    nc.scalar.copy(out=x_grouped[g][:, m, :], in_=bank)
+                    nc.scalar.copy(out=words, in_=bank)
 
             def quantise_x(g, m):
-                quantise(x_words[:, m, tokens_of(g)], x_scales[:, m, tokens_of(g)], x_grouped[g][:, m, :])
+                tokens = tokens_of_group(g)
+                quantise(x_words[:, m, tokens], x_scales[:, m, tokens], x_grouped[g][:, m, :])
 
-            def first_matmul(bank):
-                g, step = divmod(bank, STEPS)
-                m, half = divmod(step, 2)
-                h_banks[bank] = h_psum.tile([P, 2, GROUP], F32, name="h_bank", tag="h_bank")
-                for i in range(2):
-                    j = 2 * half + i
-                    matmul_mx(
-                        h_banks[bank][:, i, :],
-                        w_in_words[:, hidden(j)],
-                        w_in_scales[:, hidden(j)],
-                        x_words[:, m, tokens_of(g)],
-                        x_scales[:, m, tokens_of(g)],
-                    )
+            def first_matmul(c, m):
+                h_banks[(c, m)] = h_psum.tile([P, 512], F32, name="h_bank", tag="h_bank")
+                tokens = tokens_of_chunk(c)
+                matmul_mx(
+                    h_banks[(c, m)][:], x_words[:, m, tokens], x_scales[:, m, tokens], w_in_words[:], w_in_scales[:]
+                )
 
-            def square(bank):
-                g, step = divmod(bank, STEPS)
-                m, half = divmod(step, 2)
-                if step == 0:
-                    squares[g] = square_pool.tile([P, 3, 4, GROUP], F32, name="squares", tag="squares")
+            def square(c, m):
+                if m == 0:
+                    squares[c] = square_pool.tile([P, 3, 512], F32, name="squares", tag="squares")
+                nc.scalar.activation(out=squares[c][:, m, :], in_=h_banks[(c, m)][:], func=ACT.Square)
+
+            def sum_squares(c):
+                sums[c] = sum_psum.tile([P, 4, CHUNK], F32, name="sums", tag="sums")
+                for j in range(4):
+                    for m in range(3):
+                        nc.tensor.matmul(
+                            sums[c][:, j, :],
+                            lhsT=squares[c][:, m, hidden(j)],
+                            rhs=identity[:],
+                            start=m == 0,
+                            stop=m == 2,
+                            is_transpose=True,
+                        )
+
+            def inverse_root(c):
                 nc.scalar.activation(
-                    out=squares[g][:, m, 2 * half : 2 * half + 2, :], in_=h_banks[bank][:], func=ACT.Square
+                    out=factors[:, :, tokens_of_chunk(c)], in_=sums[c][:], func=ACT.Abs_reciprocal_sqrt
                 )
 
-            def add_first_two(g):
-                nc.vector.tensor_tensor(
-                    out=squares[g][:, 0, :, :], in0=squares[g][:, 0, :, :], in1=squares[g][:, 1, :, :], op=ALU.add
-                )
-
-            def add_third(g):
-                nc.vector.tensor_tensor(
-                    out=norms[:, :, tokens_of(g)], in0=squares[g][:, 0, :, :], in1=squares[g][:, 2, :, :], op=ALU.add
-                )
-
-            def inverse_root(g):
-                nc.scalar.activation(
-                    out=factors[:, :, tokens_of(g)], in_=norms[:, :, tokens_of(g)], func=ACT.Abs_reciprocal_sqrt
-                )
-
-            def norm(g):
+            def norm(c):
                 nc.vector.scalar_tensor_tensor(
-                    out=norms[:, :, tokens_of(g)],
-                    in0=factors[:, :, tokens_of(g)],
+                    out=norms[:, :, tokens_of_chunk(c)],
+                    in0=factors[:, :, tokens_of_chunk(c)],
                     scalar=MAX_INV_NORM,
-                    in1=norms[:, :, tokens_of(g)],
+                    in1=sums[c][:],
                     op0=ALU.min,
                     op1=ALU.mult,
                 )
@@ -166,7 +175,10 @@ def tile_feedforwardse3_pa_t_kernel(tc, x, w_in, scale, bias, w_out, out):
             w_in_rows = w_pool.tile([P, 4, 512], BF16, name="w_in_rows")
             w_in_grouped = w_pool.tile([P, 512, 4], BF16, name="w_in_grouped", align_bytes=64)
             load_x(0)
-            nc.sync.dma_start(out=w_in_rows[:], in_=w_in.rearrange("(j p) f -> p j f", p=P))
+            nc.sync.dma_start(
+                out=w_in_rows[:].rearrange("p (u e) f -> p u (e f)", u=2),
+                in_=w_in.rearrange("(u p e) f -> p u (e f)", u=2, e=2),
+            )
             nc.scalar.dma_start(out=scale_bf[:], in_=scale.rearrange("a b (p j) -> (a b p) j", j=4))
             nc.scalar.dma_start(out=bias_bf[:], in_=bias.rearrange("a b (p j) -> (a b p) j", j=4))
             make_identity(nc, identity[:])
@@ -175,6 +187,8 @@ def tile_feedforwardse3_pa_t_kernel(tc, x, w_in, scale, bias, w_out, out):
             for g in range(1, X_TILES):
                 load_x(g)
 
+            for m in range(3):
+                part_x(0, m)
             sorted_rows = w_in_rows[:].rearrange("p j (b a) -> p a b j", a=4)
             sorted_grouped = w_in_grouped[:].rearrange("p (a b) j -> p a b j", a=4)
             nc.vector.tensor_copy(out=sorted_grouped[:, 0:2, :, :], in_=sorted_rows[:, 0:2, :, :])
@@ -182,45 +196,45 @@ def tile_feedforwardse3_pa_t_kernel(tc, x, w_in, scale, bias, w_out, out):
             nc.scalar.copy(out=scale_f32[:], in_=scale_bf[:])
             nc.scalar.copy(out=bias_f32[:], in_=bias_bf[:])
 
-            for g in range(-2, N_GROUPS + 1):
-                for step in range(STEPS):
-                    bank = STEPS * g + step
-                    if step == 0 and is_group(g - 1):
-                        add_third(g - 1)
-                    if step == 0 and is_group(g + 1):
-                        copy_x(g + 1, 0)
-                    if step == 0 and is_group(g - 2) and g - 2 < N_GROUPS - 2:
-                        norm(g - 2)
-                    if step == 0 and g + 1 == 0:
-                        quantise(w_in_words[:], w_in_scales[:], w_in_grouped[:].rearrange("p c j -> p (c j)"))
-                    if step in (1, 2) and is_group(g + 1):
-                        quantise_x(g + 1, step - 1)
-                    if step == 4 and is_group(g):
-                        add_first_two(g)
-                    if step == 4 and is_group(g + 1):
-                        quantise_x(g + 1, 2)
+            for c in range(-3, N_CHUNKS + 2):
+                odd = c % 2 == 1
+                g = (c + 3) // 2
+                if is_chunk(c - 1):
+                    sum_squares(c - 1)
+                if odd:
+                    if is_group(g - 1):
+                        quantise_x(g - 1, 2)
+                elif is_group(g):
+                    quantise_x(g, 0)
+                    quantise_x(g, 1)
+                if c == -2:
+                    quantise(w_in_words[:], w_in_scales[:], w_in_grouped[:].rearrange("p c j -> p (c j)"))
+                if is_chunk(c - 2):
+                    norm(c - 2)
+                if odd and c > -3 and is_group(g):
+                    part_x(g, 2)
+                if not odd and is_group(g + 1):
+                    part_x(g + 1, 0)
+                    part_x(g + 1, 1)
+                for m in (0, 1) if odd else (2,):
                     if is_group(g):
-                        square(bank)
-                    if 0 <= bank + H_BANKS < STEPS * N_GROUPS:
-                        first_matmul(bank + H_BANKS)
-                    if step in (1, 2) and is_group(g + 1):
-                        copy_x(g + 1, step)
-                    if step == 2 and is_group(g + 2):
-                        transpose_x(g + 2, 0)
-                        transpose_x(g + 2, 1)
-                    if step == 4 and is_group(g + 2):
-                        transpose_x(g + 2, 2)
-                        if g + 2 + X_TILES < N_GROUPS:
-                            load_x(g + 2 + X_TILES)
-                        if g + 2 == N_GROUPS - 1:
-                            nc.sync.dma_start(out=w_out_rows[:], in_=w_out.rearrange("(p j) d -> p j d", j=4))
-                    if step == 3 and is_group(g - 1) and g - 1 < N_GROUPS - 2:
-                        inverse_root(g - 1)
-            inverse_root(N_GROUPS - 2)
-            norm(N_GROUPS - 2)
-            inverse_root(N_GROUPS - 1)
+                        transpose_x(g, m)
+                        if m in VECTOR_COPIES_M:
+                            copy_x(g, m)
+                if not odd and is_group(g) and g + X_TILES < N_GROUPS:
+                    load_x(g + X_TILES)
+                if c == N_CHUNKS - 6:
+                    nc.sync.dma_start(out=w_out_rows[:], in_=w_out.rearrange("(p j) d -> p j d", j=4))
+                for m in range(3):
+                    if is_chunk(c):
+                        square(c, m)
+                    if is_chunk(c + 1):
+                        first_matmul(c + 1, m)
+                if is_chunk(c - 1):
+                    inverse_root(c - 1)
+                if odd and is_group(g):
+                    copy_x(g, 1)
             nc.vector.tensor_copy(out=w_out_grouped[:], in_=w_out_rows[:].rearrange("p j d -> p d j"))
-            norm(N_GROUPS - 1)
             quantise(w_out_words[:], w_out_scales[:], w_out_grouped[:].rearrange("p c j -> p (c j)"))
 
         with ExitStack() as part2:

@@ -239,13 +239,11 @@ def tile_feedforwardse3_pa_t_kernel(tc, x, w_in, scale, bias, w_out, out):
 
         with ExitStack() as part2:
             g_pool = part2.enter_context(tc.tile_pool(name="g_pool", bufs=3))
-            factor_pool = part2.enter_context(tc.tile_pool(name="factor_pool", bufs=4))
             out_pool = part2.enter_context(tc.tile_pool(name="out_pool", bufs=6))
             h_again_psum = part2.enter_context(tc.psum_pool(name="h_again_psum", bufs=4))
             out_psum = part2.enter_context(tc.psum_pool(name="out_psum", bufs=4))
 
             h_again = {}
-            chunk_factors = {}
 
             def gelu(first, count, j):
                 nc.scalar.activation(
@@ -258,17 +256,14 @@ def tile_feedforwardse3_pa_t_kernel(tc, x, w_in, scale, bias, w_out, out):
 
             def factor(first, count):
                 span = slice(first, first + count)
-                tile = factor_pool.tile([P, 2 * CHUNK, 4], F32, name="factor_tile", tag="factor_tile")
                 nc.vector.scalar_tensor_tensor(
-                    out=tile[:, 0:count, :],
-                    in0=factors[:, :, span].rearrange("p j t -> p t j"),
+                    out=factors[:, :, span],
+                    in0=factors[:, :, span],
                     scalar=MAX_INV_NORM,
-                    in1=norms[:, :, span].rearrange("p j t -> p t j"),
+                    in1=norms[:, :, span],
                     op0=ALU.min,
                     op1=ALU.mult,
                 )
-                for k in range(count // CHUNK):
-                    chunk_factors[first // CHUNK + k] = tile[:, CHUNK * k : CHUNK * (k + 1), :]
 
             def first_matmul_again(c, m):
                 tokens = slice(CHUNK * c, CHUNK * (c + 1))
@@ -298,11 +293,12 @@ def tile_feedforwardse3_pa_t_kernel(tc, x, w_in, scale, bias, w_out, out):
                 g_grouped = g_pool.tile([P, 3, CHUNK, 4], BF16, name="g_grouped", tag="g_grouped", align_bytes=64)
                 g_words = g_pool.tile([P, 3 * CHUNK], U32, name="g_words", tag="g_words", align_bytes=64)
                 g_scales = g_pool.tile([P, 3 * CHUNK], U8, name="g_scales", tag="g_scales", align_bytes=64)
+                chunk_factors = factors[:, :, CHUNK * c : CHUNK * (c + 1)].rearrange("p j (q i) -> p q j i", i=4)
                 for m in range(3):
                     nc.vector.tensor_tensor(
-                        out=g_grouped[:, m, :, :],
-                        in0=h_again[(c, m)][:].rearrange("p j t -> p t j"),
-                        in1=chunk_factors[c],
+                        out=g_grouped[:, m, :, :].rearrange("p (q i) j -> p q j i", i=4),
+                        in0=h_again[(c, m)][:].rearrange("p j (q i) -> p q j i", i=4),
+                        in1=chunk_factors,
                         op=ALU.mult,
                     )
                     if m < 2 and not last:

@@ -67,6 +67,10 @@ def tile_feedforwardse3_pa_t_kernel(tc, x, w_in, scale, bias, w_out, out):
                 stop=True,
             )
 
+        def clamp(first, end):
+            span = slice(CHUNK * first, CHUNK * end)
+            nc.vector.tensor_scalar_min(out=factors[:, :, span], in0=factors[:, :, span], scalar1=MAX_INV_NORM)
+
         def hidden(j):
             return slice(P * j, P * (j + 1))
 
@@ -88,6 +92,9 @@ def tile_feedforwardse3_pa_t_kernel(tc, x, w_in, scale, bias, w_out, out):
             squares = {}
             sums = {}
 
+            def by_vector(g, m):
+                return m != 1
+
             def is_group(g):
                 return 0 <= g < N_GROUPS
 
@@ -100,9 +107,11 @@ def tile_feedforwardse3_pa_t_kernel(tc, x, w_in, scale, bias, w_out, out):
             def tokens_of_chunk(c):
                 return slice(CHUNK * c, CHUNK * (c + 1))
 
-            def load_x(g):
-                x_rows[g] = x_pool.tile([P, UNITS, 768], BF16, name="x_rows", tag="x_rows")
-                nc.sync.dma_start(out=x_rows[g][:], in_=x_units[:, UNITS * g : UNITS * (g + 1), :])
+            def load_x(g, first=0, end=UNITS):
+                if first == 0:
+                    x_rows[g] = x_pool.tile([P, UNITS, 768], BF16, name="x_rows", tag="x_rows")
+                units = slice(UNITS * g + first, UNITS * g + end)
+                nc.sync.dma_start(out=x_rows[g][:, first:end, :], in_=x_units[:, units, :])
 
             def part_x(g, m):
                 if m == 0:
@@ -123,7 +132,7 @@ def tile_feedforwardse3_pa_t_kernel(tc, x, w_in, scale, bias, w_out, out):
                     )
                 words = x_grouped[g][:, m, :].bitcast(F32)
                 bank = x_transposed[(g, m)][:].rearrange("p u c -> p (u c)")
-                if m in VECTOR_COPIES_M:
+                if by_vector(g, m):
                     nc.vector.tensor_copy(out=words, in_=bank)
                 else:
                     nc.scalar.copy(out=words, in_=bank)
@@ -174,7 +183,7 @@ def tile_feedforwardse3_pa_t_kernel(tc, x, w_in, scale, bias, w_out, out):
 
             w_in_rows = w_pool.tile([P, 4, 512], BF16, name="w_in_rows")
             w_in_grouped = w_pool.tile([P, 512, 4], BF16, name="w_in_grouped", align_bytes=64)
-            load_x(0)
+            load_x(0, 0, 2)
             nc.sync.dma_start(
                 out=w_in_rows[:].rearrange("p (u e) f -> p u (e f)", u=2),
                 in_=w_in.rearrange("(u p e) f -> p u (e f)", u=2, e=2),
@@ -184,34 +193,105 @@ def tile_feedforwardse3_pa_t_kernel(tc, x, w_in, scale, bias, w_out, out):
             make_identity(nc, identity[:])
             nc.vector.memset(one[:], 1.0)
             nc.scalar.activation(out=unused[:], in_=one[:], func=ACT.Abs_reciprocal_sqrt)
+            load_x(0, 2, UNITS)
             for g in range(1, X_TILES):
                 load_x(g)
 
-            for m in range(3):
-                part_x(0, m)
+            x_planes[0] = plane_pool.tile([P, 3, UNITS, 256], BF16, name="x_planes", tag="x_planes")
+            x_grouped[0] = grouped_pool.tile([P, 3, 4 * GROUP], BF16, name="x_grouped", tag="x_grouped", align_bytes=64)
+            rows_0 = x_rows[0][:].rearrange("p u (d m) -> p u d m", m=3)
+            half_banks = {}
+
+            def part_half(half):
+                units = slice(2 * half, 2 * half + 2)
+                for m in range(2):
+                    nc.vector.tensor_copy(out=x_planes[0][:, m, units, :], in_=rows_0[:, units, :, m])
+                nc.scalar.copy(out=x_planes[0][:, 2, units, :], in_=rows_0[:, units, :, 2])
+
+            def transpose_half(half):
+                for bank in range(2):
+                    half_banks[bank] = xt_psum.tile([P, UNITS, P], F32, name="x_transposed", tag="x_transposed")
+                for m in range(3):
+                    for u in range(2):
+                        words = x_planes[0][:, m, 2 * half + u, :].bitcast(F32)
+                        nc.tensor.transpose(half_banks[m // 2][:, 2 * (m % 2) + u, :], words, identity[:])
+
+            def copy_half(half):
+                values = x_grouped[0][:, :, 4 * CHUNK * half : 4 * CHUNK * (half + 1)].bitcast(F32)
+                nc.vector.tensor_copy(
+                    out=values[:, 0:2, :], in_=half_banks[0][:].rearrange("p (m u) c -> p m (u c)", m=2)
+                )
+                nc.scalar.copy(out=values[:, 2, :], in_=half_banks[1][:, 0:2, :].rearrange("p u c -> p (u c)"))
+
+            def quantise_half(half, m):
+                tokens = tokens_of_chunk(half)
+                values = x_grouped[0][:, m, 4 * CHUNK * half : 4 * CHUNK * (half + 1)]
+                quantise(x_words[:, m, tokens], x_scales[:, m, tokens], values)
+
+            part_half(0)
+            transpose_half(0)
             sorted_rows = w_in_rows[:].rearrange("p j (b a) -> p a b j", a=4)
             sorted_grouped = w_in_grouped[:].rearrange("p (a b) j -> p a b j", a=4)
+            copy_half(0)
             nc.vector.tensor_copy(out=sorted_grouped[:, 0:2, :, :], in_=sorted_rows[:, 0:2, :, :])
             nc.scalar.copy(out=sorted_grouped[:, 2:4, :, :], in_=sorted_rows[:, 2:4, :, :])
+            quantise_half(0, 0)
+            quantise_half(0, 1)
+            quantise(w_in_words[:], w_in_scales[:], w_in_grouped[:].rearrange("p c j -> p (c j)"))
+            quantise_half(0, 2)
+            for m in range(3):
+                first_matmul(0, m)
+            part_half(1)
+            load_x(X_TILES)
+            transpose_half(1)
+            part_x(1, 0)
+            part_x(1, 1)
+            square(0, 0)
+            copy_half(1)
+            for m in range(3):
+                quantise_half(1, m)
+            square(0, 1)
+            square(0, 2)
+            for m in range(2):
+                transpose_x(1, m)
+            for m in range(3):
+                first_matmul(1, m)
+            copy_x(1, 0)
+            part_x(1, 2)
+            copy_x(1, 1)
             nc.scalar.copy(out=scale_f32[:], in_=scale_bf[:])
             nc.scalar.copy(out=bias_f32[:], in_=bias_bf[:])
 
-            for c in range(-3, N_CHUNKS + 2):
+            def arrange_w_out():
+                nc.vector.tensor_copy(out=w_out_grouped[:], in_=w_out_rows[:].rearrange("p j d -> p d j"))
+
+            def quantise_w_out():
+                quantise(w_out_words[:], w_out_scales[:], w_out_grouped[:].rearrange("p c j -> p (c j)"))
+                clamp(13, 16)
+
+            late_work = {
+                12: lambda: clamp(10, 13),
+                13: arrange_w_out,
+                14: lambda: clamp(0, 10),
+                15: quantise_w_out,
+            }
+
+            for c in range(N_CHUNKS + 2):
                 odd = c % 2 == 1
                 g = (c + 3) // 2
                 if is_chunk(c - 1):
                     sum_squares(c - 1)
+                if is_chunk(c - 2):
+                    norm(c - 2)
+                if c - 2 in late_work:
+                    late_work[c - 2]()
                 if odd:
                     if is_group(g - 1):
                         quantise_x(g - 1, 2)
                 elif is_group(g):
                     quantise_x(g, 0)
                     quantise_x(g, 1)
-                if c == -2:
-                    quantise(w_in_words[:], w_in_scales[:], w_in_grouped[:].rearrange("p c j -> p (c j)"))
-                if is_chunk(c - 2):
-                    norm(c - 2)
-                if odd and c > -3 and is_group(g):
+                if odd and is_group(g):
                     part_x(g, 2)
                 if not odd and is_group(g + 1):
                     part_x(g + 1, 0)
@@ -219,24 +299,23 @@ def tile_feedforwardse3_pa_t_kernel(tc, x, w_in, scale, bias, w_out, out):
                 for m in (0, 1) if odd else (2,):
                     if is_group(g):
                         transpose_x(g, m)
-                        if m in VECTOR_COPIES_M:
+                        if by_vector(g, m):
                             copy_x(g, m)
                 if not odd and is_group(g) and g + X_TILES < N_GROUPS:
                     load_x(g + X_TILES)
                 if c == N_CHUNKS - 6:
                     nc.sync.dma_start(out=w_out_rows[:], in_=w_out.rearrange("(p j) d -> p j d", j=4))
                 for m in range(3):
-                    if is_chunk(c):
+                    if 0 < c < N_CHUNKS:
                         square(c, m)
-                    if is_chunk(c + 1):
-                        first_matmul(c + 1, m)
+                        if is_chunk(c + 1):
+                            first_matmul(c + 1, m)
                 if is_chunk(c - 1):
                     inverse_root(c - 1)
-                if odd and is_group(g):
-                    copy_x(g, 1)
-            nc.vector.tensor_copy(out=w_out_grouped[:], in_=w_out_rows[:].rearrange("p j d -> p d j"))
-            quantise(w_out_words[:], w_out_scales[:], w_out_grouped[:].rearrange("p c j -> p (c j)"))
-
+                if is_group(g):
+                    for m in (0, 1) if odd else (2,):
+                        if not by_vector(g, m):
+                            copy_x(g, m)
         with ExitStack() as part2:
             g_pool = part2.enter_context(tc.tile_pool(name="g_pool", bufs=3))
             out_pool = part2.enter_context(tc.tile_pool(name="out_pool", bufs=6))
@@ -244,6 +323,7 @@ def tile_feedforwardse3_pa_t_kernel(tc, x, w_in, scale, bias, w_out, out):
             out_psum = part2.enter_context(tc.psum_pool(name="out_psum", bufs=4))
 
             h_again = {}
+            chunk_factors = {}
 
             def gelu(first, count, j):
                 nc.scalar.activation(
@@ -254,16 +334,14 @@ def tile_feedforwardse3_pa_t_kernel(tc, x, w_in, scale, bias, w_out, out):
                     scale=scale_f32[:, j : j + 1],
                 )
 
-            def factor(first, count):
-                span = slice(first, first + count)
-                nc.vector.scalar_tensor_tensor(
-                    out=factors[:, :, span],
-                    in0=factors[:, :, span],
-                    scalar=MAX_INV_NORM,
-                    in1=norms[:, :, span],
-                    op0=ALU.min,
-                    op1=ALU.mult,
+            def chunk_factor_tile(c):
+                chunk_factors[c] = g_pool.tile(
+                    [P, 4, CHUNK], F32, name="chunk_factor", tag="g_or_factor", align_bytes=64
                 )
+                return chunk_factors[c]
+
+            def tokens_of(values, c):
+                return values[:, :, CHUNK * c : CHUNK * (c + 1)]
 
             def first_matmul_again(c, m):
                 tokens = slice(CHUNK * c, CHUNK * (c + 1))
@@ -283,26 +361,34 @@ def tile_feedforwardse3_pa_t_kernel(tc, x, w_in, scale, bias, w_out, out):
                 for j in range(4):
                     gelu(first, count, j)
                 if first == 0:
-                    factor(0, CHUNK)
+                    nc.vector.tensor_tensor(
+                        out=chunk_factor_tile(0)[:], in0=tokens_of(factors, 0), in1=tokens_of(norms, 0), op=ALU.mult
+                    )
             later_gelus = [(first, j) for first in (1024, 1536) for j in range(4)]
 
             for c in range(N_CHUNKS):
                 last = c == N_CHUNKS - 1
                 if not last:
                     first_matmul_again(c + 1, 0)
-                g_grouped = g_pool.tile([P, 3, CHUNK, 4], BF16, name="g_grouped", tag="g_grouped", align_bytes=64)
+                g_grouped = g_pool.tile([P, 3, CHUNK, 4], BF16, name="g_grouped", tag="g_or_factor", align_bytes=64)
                 g_words = g_pool.tile([P, 3 * CHUNK], U32, name="g_words", tag="g_words", align_bytes=64)
                 g_scales = g_pool.tile([P, 3 * CHUNK], U8, name="g_scales", tag="g_scales", align_bytes=64)
-                chunk_factors = factors[:, :, CHUNK * c : CHUNK * (c + 1)].rearrange("p j (q i) -> p q j i", i=4)
                 for m in range(3):
                     nc.vector.tensor_tensor(
                         out=g_grouped[:, m, :, :].rearrange("p (q i) j -> p q j i", i=4),
-                        in0=h_again[(c, m)][:].rearrange("p j (q i) -> p q j i", i=4),
-                        in1=chunk_factors,
+                        in0=chunk_factors[c][:].rearrange("p j (q i) -> p q j i", i=4),
+                        in1=h_again[(c, m)][:].rearrange("p j (q i) -> p q j i", i=4),
                         op=ALU.mult,
                     )
                     if m < 2 and not last:
                         first_matmul_again(c + 1, m + 1)
+                if not last:
+                    nc.gpsimd.tensor_tensor(
+                        out=chunk_factor_tile(c + 1)[:],
+                        in0=tokens_of(factors, c + 1),
+                        in1=tokens_of(norms, c + 1),
+                        op=ALU.mult,
+                    )
                 quantise(
                     g_words[:, 0 : 2 * CHUNK],
                     g_scales[:, 0 : 2 * CHUNK],
@@ -313,11 +399,6 @@ def tile_feedforwardse3_pa_t_kernel(tc, x, w_in, scale, bias, w_out, out):
                     g_scales[:, 2 * CHUNK : 3 * CHUNK],
                     g_grouped[:, 2, :, :].rearrange("p t j -> p (t j)"),
                 )
-                if c == 0:
-                    factor(CHUNK, CHUNK)
-                if c % 2 == 0 and c + 2 < N_CHUNKS:
-                    factor(CHUNK * (c + 2), 2 * CHUNK)
-
                 out_rows = out_pool.tile([P, ROW], F32, name="out_rows", tag="out_rows")
                 for quarter in range(4):
                     channels = slice(P * quarter, P * (quarter + 1))
@@ -335,11 +416,10 @@ def tile_feedforwardse3_pa_t_kernel(tc, x, w_in, scale, bias, w_out, out):
                         nc.vector.tensor_copy(out=interleaved, in_=acc[:].rearrange("p m d -> p d m"))
                     else:
                         nc.scalar.copy(out=interleaved, in_=acc[:].rearrange("p m d -> p d m"))
-                    if last and quarter == 1:
-                        nc.sync.dma_start(out=out_chunks[:, c, 0 : ROW // 2], in_=out_rows[:, 0 : ROW // 2])
-                if last:
-                    nc.sync.dma_start(out=out_chunks[:, c, ROW // 2 : ROW], in_=out_rows[:, ROW // 2 : ROW])
-                else:
+                    if last:
+                        part = slice(384 * quarter, 384 * (quarter + 1))
+                        nc.sync.dma_start(out=out_chunks[:, c, part], in_=out_rows[:, part])
+                if not last:
                     nc.sync.dma_start(out=out_chunks[:, c, :], in_=out_rows[:])
                 if c < len(later_gelus):
                     gelu(later_gelus[c][0], 512, later_gelus[c][1])

@@ -22,6 +22,7 @@ N_CHUNKS = TOKENS // CHUNK
 N_GROUPS = TOKENS // GROUP
 UNITS = 4
 X_TILES = 4
+CLAMP_AFTER = (11, 12, 14, 15)
 MAX_INV_NORM = 1.0e12
 VECTOR_COPIES_M = (0, 2)
 
@@ -233,8 +234,16 @@ def tile_feedforwardse3_pa_t_kernel(tc, x, w_in, scale, bias, w_out, out):
             sorted_rows = w_in_rows[:].rearrange("p j (b a) -> p a b j", a=4)
             sorted_grouped = w_in_grouped[:].rearrange("p (a b) j -> p a b j", a=4)
             copy_half(0)
+            nc.gpsimd.tensor_scalar(
+                out=sorted_grouped[:, 3, :, :],
+                in0=sorted_rows[:, 3, :, :],
+                scalar1=1.0,
+                scalar2=0.0,
+                op0=ALU.mult,
+                op1=ALU.add,
+            )
             nc.vector.tensor_copy(out=sorted_grouped[:, 0:2, :, :], in_=sorted_rows[:, 0:2, :, :])
-            nc.scalar.copy(out=sorted_grouped[:, 2:4, :, :], in_=sorted_rows[:, 2:4, :, :])
+            nc.scalar.copy(out=sorted_grouped[:, 2, :, :], in_=sorted_rows[:, 2, :, :])
             quantise_half(0, 0)
             quantise_half(0, 1)
             quantise(w_in_words[:], w_in_scales[:], w_in_grouped[:].rearrange("p c j -> p (c j)"))
@@ -262,19 +271,14 @@ def tile_feedforwardse3_pa_t_kernel(tc, x, w_in, scale, bias, w_out, out):
             nc.scalar.copy(out=scale_f32[:], in_=scale_bf[:])
             nc.scalar.copy(out=bias_f32[:], in_=bias_bf[:])
 
-            def arrange_w_out():
-                nc.vector.tensor_copy(out=w_out_grouped[:], in_=w_out_rows[:].rearrange("p j d -> p d j"))
-
-            def quantise_w_out():
-                quantise(w_out_words[:], w_out_scales[:], w_out_grouped[:].rearrange("p c j -> p (c j)"))
-                clamp(13, 16)
-
-            late_work = {
-                12: lambda: clamp(10, 13),
-                13: arrange_w_out,
-                14: lambda: clamp(0, 10),
-                15: quantise_w_out,
-            }
+            def late_work(c):
+                if c in CLAMP_AFTER:
+                    first = 4 * CLAMP_AFTER.index(c)
+                    clamp(first, first + 4)
+                if c == N_CHUNKS - 3:
+                    nc.vector.tensor_copy(out=w_out_grouped[:], in_=w_out_rows[:].rearrange("p j d -> p d j"))
+                if c == N_CHUNKS - 2:
+                    quantise(w_out_words[:], w_out_scales[:], w_out_grouped[:].rearrange("p c j -> p (c j)"))
 
             for c in range(N_CHUNKS + 2):
                 odd = c % 2 == 1
@@ -283,8 +287,6 @@ def tile_feedforwardse3_pa_t_kernel(tc, x, w_in, scale, bias, w_out, out):
                     sum_squares(c - 1)
                 if is_chunk(c - 2):
                     norm(c - 2)
-                if c - 2 in late_work:
-                    late_work[c - 2]()
                 if odd:
                     if is_group(g - 1):
                         quantise_x(g - 1, 2)
@@ -301,6 +303,7 @@ def tile_feedforwardse3_pa_t_kernel(tc, x, w_in, scale, bias, w_out, out):
                         transpose_x(g, m)
                         if by_vector(g, m):
                             copy_x(g, m)
+                late_work(c - 2)
                 if not odd and is_group(g) and g + X_TILES < N_GROUPS:
                     load_x(g + X_TILES)
                 if c == N_CHUNKS - 6:

@@ -94,7 +94,7 @@ def tile_feedforwardse3_pa_t_kernel(tc, x, w_in, scale, bias, w_out, out):
             sums = {}
 
             def by_vector(g, m):
-                return m != 1
+                return m != 1 and not (g == 1 and m == 0)
 
             def is_group(g):
                 return 0 <= g < N_GROUPS
@@ -155,7 +155,10 @@ def tile_feedforwardse3_pa_t_kernel(tc, x, w_in, scale, bias, w_out, out):
                 nc.scalar.activation(out=squares[c][:, m, :], in_=h_banks[(c, m)][:], func=ACT.Square)
 
             def sum_squares(c):
-                sums[c] = sum_psum.tile([P, 4, CHUNK], F32, name="sums", tag="sums")
+                if c == N_CHUNKS - 1:
+                    sums[c] = xt_psum.tile([P, UNITS, P], F32, name="x_transposed", tag="x_transposed")
+                else:
+                    sums[c] = sum_psum.tile([P, 4, CHUNK], F32, name="sums", tag="sums")
                 for j in range(4):
                     for m in range(3):
                         nc.tensor.matmul(
@@ -267,26 +270,36 @@ def tile_feedforwardse3_pa_t_kernel(tc, x, w_in, scale, bias, w_out, out):
                 first_matmul(1, m)
             copy_x(1, 0)
             part_x(1, 2)
+            part_x(2, 0)
+            part_x(2, 1)
             copy_x(1, 1)
             nc.scalar.copy(out=scale_f32[:], in_=scale_bf[:])
             nc.scalar.copy(out=bias_f32[:], in_=bias_bf[:])
 
             def late_work(c):
-                if c in CLAMP_AFTER:
-                    first = 4 * CLAMP_AFTER.index(c)
-                    clamp(first, first + 4)
-                if c == N_CHUNKS - 3:
+                if c in (5, 7, 9, 11):
+                    clamp((c - 5) // 2, (c - 3) // 2)
+                if c == 13:
+                    clamp(4, 7)
+                if c == 14:
+                    clamp(7, 10)
+                if c == 15:
                     nc.vector.tensor_copy(out=w_out_grouped[:], in_=w_out_rows[:].rearrange("p j d -> p d j"))
-                if c == N_CHUNKS - 2:
+                    clamp(10, 13)
                     quantise(w_out_words[:], w_out_scales[:], w_out_grouped[:].rearrange("p c j -> p (c j)"))
+                if c == 17:
+                    clamp(13, 16)
 
+            ROOT_SLOT = {14: [], 15: [13, 14], 16: [15]}
+            NORM_SLOT = {15: [], 16: [13], 17: [14, 15]}
             for c in range(N_CHUNKS + 2):
                 odd = c % 2 == 1
                 g = (c + 3) // 2
                 if is_chunk(c - 1):
                     sum_squares(c - 1)
-                if is_chunk(c - 2):
-                    norm(c - 2)
+                for k in NORM_SLOT.get(c, [c - 2]):
+                    if is_chunk(k):
+                        norm(k)
                 if odd:
                     if is_group(g - 1):
                         quantise_x(g - 1, 2)
@@ -296,14 +309,15 @@ def tile_feedforwardse3_pa_t_kernel(tc, x, w_in, scale, bias, w_out, out):
                 if odd and is_group(g):
                     part_x(g, 2)
                 if not odd and is_group(g + 1):
-                    part_x(g + 1, 0)
-                    part_x(g + 1, 1)
+                    if c > 0:
+                        part_x(g + 1, 0)
+                        part_x(g + 1, 1)
                 for m in (0, 1) if odd else (2,):
                     if is_group(g):
                         transpose_x(g, m)
                         if by_vector(g, m):
                             copy_x(g, m)
-                late_work(c - 2)
+                late_work(c)
                 if not odd and is_group(g) and g + X_TILES < N_GROUPS:
                     load_x(g + X_TILES)
                 if c == N_CHUNKS - 6:
@@ -313,8 +327,9 @@ def tile_feedforwardse3_pa_t_kernel(tc, x, w_in, scale, bias, w_out, out):
                         square(c, m)
                         if is_chunk(c + 1):
                             first_matmul(c + 1, m)
-                if is_chunk(c - 1):
-                    inverse_root(c - 1)
+                for k in ROOT_SLOT.get(c, [c - 1]):
+                    if is_chunk(k):
+                        inverse_root(k)
                 if is_group(g):
                     for m in (0, 1) if odd else (2,):
                         if not by_vector(g, m):

@@ -94,7 +94,7 @@ def tile_feedforwardse3_pa_t_kernel(tc, x, w_in, scale, bias, w_out, out):
             sums = {}
 
             def by_vector(g, m):
-                return m != 1 and not (g == 1 and m == 0)
+                return m == 2 or (g > 1 and (m == 0 or g % 2 == 1))
 
             def is_group(g):
                 return 0 <= g < N_GROUPS
@@ -382,7 +382,7 @@ def tile_feedforwardse3_pa_t_kernel(tc, x, w_in, scale, bias, w_out, out):
                     nc.vector.tensor_tensor(
                         out=chunk_factor_tile(0)[:], in0=tokens_of(factors, 0), in1=tokens_of(norms, 0), op=ALU.mult
                     )
-            later_gelus = [(first, j) for first in (1024, 1536) for j in range(4)]
+            later_gelus = [(first, j) for first in range(1024, TOKENS, 256) for j in range(4)]
 
             for c in range(N_CHUNKS):
                 last = c == N_CHUNKS - 1
@@ -437,7 +437,8 @@ def tile_feedforwardse3_pa_t_kernel(tc, x, w_in, scale, bias, w_out, out):
                     if last:
                         part = slice(384 * quarter, 384 * (quarter + 1))
                         nc.sync.dma_start(out=out_chunks[:, c, part], in_=out_rows[:, part])
-                if not last:
-                    nc.sync.dma_start(out=out_chunks[:, c, :], in_=out_rows[:])
-                if c < len(later_gelus):
-                    gelu(later_gelus[c][0], 512, later_gelus[c][1])
+                    elif quarter % 2 == 1:
+                        part = slice(384 * (quarter - 1), 384 * (quarter + 1))
+                        nc.sync.dma_start(out=out_chunks[:, c, part], in_=out_rows[:, part])
+                for first, j in later_gelus[3 * c // 2 : 3 * (c + 1) // 2]:
+                    gelu(first, 256, j)

from contextlib import ExitStack

import concourse.mybir as mybir
from concourse.masks import make_identity

FLOPS = 2 * 2 * 2048 * 3 * 512 * 512

BF16 = mybir.dt.bfloat16
F32 = mybir.dt.float32
U32 = mybir.dt.uint32
U8 = mybir.dt.uint8
FP8X4 = mybir.dt.float8_e4m3fn_x4
ACT = mybir.ActivationFunctionType
ALU = mybir.AluOpType

P = 128
TOKENS = 2048
ROW = 1536
CHUNK = 128
GROUP = 256
N_CHUNKS = TOKENS // CHUNK
N_GROUPS = TOKENS // GROUP
UNITS = 4
X_TILES = 4
CLAMP_AFTER = (11, 12, 14, 15)
MAX_INV_NORM = 1.0e12
VECTOR_COPIES_M = (0, 2)


def tile_feedforwardse3_pa_t_kernel(tc, x, w_in, scale, bias, w_out, out):
    nc = tc.nc
    x_units = x.rearrange("b n (h d) m -> (b n h) (d m)", h=2).rearrange("(u p) e -> p u e", p=P)
    out_chunks = out.rearrange("b n d m -> (b n) (d m)").rearrange("(c p) e -> p c e", p=P)

    with ExitStack() as ctx:
        ctx.enter_context(tc.manual_schedule())
        keep = ctx.enter_context(tc.tile_pool(name="keep", bufs=1))

        identity = keep.tile([P, P], F32, name="identity")
        w_in_words = keep.tile([P, 512], U32, name="w_in_words", align_bytes=64)
        w_in_scales = keep.tile([P, 512], U8, name="w_in_scales", align_bytes=64)
        w_out_words = keep.tile([P, 512], U32, name="w_out_words", align_bytes=64)
        w_out_scales = keep.tile([P, 512], U8, name="w_out_scales", align_bytes=64)
        x_words = keep.tile([P, 3, TOKENS], U32, name="x_words", align_bytes=64)
        x_scales = keep.tile([P, 3, TOKENS], U8, name="x_scales", align_bytes=64)
        w_out_rows = keep.tile([P, 4, 512], BF16, name="w_out_rows")
        w_out_grouped = keep.tile([P, 512, 4], BF16, name="w_out_grouped", align_bytes=64)
        norms = keep.tile([P, 4, TOKENS], F32, name="norms")
        factors = keep.tile([P, 4, TOKENS], F32, name="factors")
        scale_bf = keep.tile([P, 4], BF16, name="scale_bf")
        bias_bf = keep.tile([P, 4], BF16, name="bias_bf")
        scale_f32 = keep.tile([P, 4], F32, name="scale_f32")
        bias_f32 = keep.tile([P, 4], F32, name="bias_f32")
        one = keep.tile([P, 1], F32, name="one")
        unused = keep.tile([P, 1], F32, name="unused")

        def quantise(words, scales, values):
            nc.vector.quantize_mx(out=words.bitcast(FP8X4), scales=scales, in_=values)

        def matmul_mx(acc, lhs_words, lhs_scales, rhs_words, rhs_scales):
            nc.tensor.matmul_mx(
                out=acc,
                lhsT=lhs_words.bitcast(FP8X4),
                lhsT_scale=lhs_scales,
                rhs=rhs_words.bitcast(FP8X4),
                rhs_scale=rhs_scales,
                start=True,
                stop=True,
            )

        def clamp(first, end):
            span = slice(CHUNK * first, CHUNK * end)
            nc.vector.tensor_scalar_min(out=factors[:, :, span], in0=factors[:, :, span], scalar1=MAX_INV_NORM)

        def hidden(j):
            return slice(P * j, P * (j + 1))

        with ExitStack() as part1:
            x_pool = part1.enter_context(tc.tile_pool(name="x_pool", bufs=X_TILES))
            plane_pool = part1.enter_context(tc.tile_pool(name="plane_pool", bufs=2))
            grouped_pool = part1.enter_context(tc.tile_pool(name="grouped_pool", bufs=2))
            square_pool = part1.enter_context(tc.tile_pool(name="square_pool", bufs=3))
            w_pool = part1.enter_context(tc.tile_pool(name="w_pool", bufs=1))
            xt_psum = part1.enter_context(tc.psum_pool(name="xt_psum", bufs=2))
            h_psum = part1.enter_context(tc.psum_pool(name="h_psum", bufs=4))
            sum_psum = part1.enter_context(tc.psum_pool(name="sum_psum", bufs=2))

            x_rows = {}
            x_planes = {}
            x_transposed = {}
            x_grouped = {}
            h_banks = {}
            squares = {}
            sums = {}

            def by_vector(g, m):
                return m == 2 or (g > 1 and (m == 0 or g % 2 == 1))

            def is_group(g):
                return 0 <= g < N_GROUPS

            def is_chunk(c):
                return 0 <= c < N_CHUNKS

            def tokens_of_group(g):
                return slice(GROUP * g, GROUP * (g + 1))

            def tokens_of_chunk(c):
                return slice(CHUNK * c, CHUNK * (c + 1))

            def load_x(g, first=0, end=UNITS):
                if first == 0:
                    x_rows[g] = x_pool.tile([P, UNITS, 768], BF16, name="x_rows", tag="x_rows")
                units = slice(UNITS * g + first, UNITS * g + end)
                nc.sync.dma_start(out=x_rows[g][:, first:end, :], in_=x_units[:, units, :])

            def part_x(g, m):
                if m == 0:
                    x_planes[g] = plane_pool.tile([P, 3, UNITS, 256], BF16, name="x_planes", tag="x_planes")
                rows = x_rows[g][:].rearrange("p u (d m) -> p u d m", m=3)
                nc.vector.tensor_copy(out=x_planes[g][:, m, :, :], in_=rows[:, :, :, m])

            def transpose_x(g, m):
                x_transposed[(g, m)] = xt_psum.tile([P, UNITS, P], F32, name="x_transposed", tag="x_transposed")
                for u in range(UNITS):
                    words = x_planes[g][:, m, u, :].bitcast(F32)
                    nc.tensor.transpose(x_transposed[(g, m)][:, u, :], words, identity[:])

            def copy_x(g, m):
                if m == 0:
                    x_grouped[g] = grouped_pool.tile(
                        [P, 3, 4 * GROUP], BF16, name="x_grouped", tag="x_grouped", align_bytes=64
                    )
                words = x_grouped[g][:, m, :].bitcast(F32)
                bank = x_transposed[(g, m)][:].rearrange("p u c -> p (u c)")
                if by_vector(g, m):
                    nc.vector.tensor_copy(out=words, in_=bank)
                else:
                    nc.scalar.copy(out=words, in_=bank)

            def quantise_x(g, m):
                tokens = tokens_of_group(g)
                quantise(x_words[:, m, tokens], x_scales[:, m, tokens], x_grouped[g][:, m, :])

            def first_matmul(c, m):
                h_banks[(c, m)] = h_psum.tile([P, 512], F32, name="h_bank", tag="h_bank")
                tokens = tokens_of_chunk(c)
                matmul_mx(
                    h_banks[(c, m)][:], x_words[:, m, tokens], x_scales[:, m, tokens], w_in_words[:], w_in_scales[:]
                )

            def square(c, m):
                if m == 0:
                    squares[c] = square_pool.tile([P, 3, 512], F32, name="squares", tag="squares")
                nc.scalar.activation(out=squares[c][:, m, :], in_=h_banks[(c, m)][:], func=ACT.Square)

            def sum_squares(c):
                if c == N_CHUNKS - 1:
                    sums[c] = xt_psum.tile([P, UNITS, P], F32, name="x_transposed", tag="x_transposed")
                else:
                    sums[c] = sum_psum.tile([P, 4, CHUNK], F32, name="sums", tag="sums")
                for j in range(4):
                    for m in range(3):
                        nc.tensor.matmul(
                            sums[c][:, j, :],
                            lhsT=squares[c][:, m, hidden(j)],
                            rhs=identity[:],
                            start=m == 0,
                            stop=m == 2,
                            is_transpose=True,
                        )

            def inverse_root(c):
                nc.scalar.activation(
                    out=factors[:, :, tokens_of_chunk(c)], in_=sums[c][:], func=ACT.Abs_reciprocal_sqrt
                )

            def norm(c):
                nc.vector.scalar_tensor_tensor(
                    out=norms[:, :, tokens_of_chunk(c)],
                    in0=factors[:, :, tokens_of_chunk(c)],
                    scalar=MAX_INV_NORM,
                    in1=sums[c][:],
                    op0=ALU.min,
                    op1=ALU.mult,
                )

            w_in_rows = w_pool.tile([P, 4, 512], BF16, name="w_in_rows")
            w_in_grouped = w_pool.tile([P, 512, 4], BF16, name="w_in_grouped", align_bytes=64)
            load_x(0, 0, 2)
            nc.sync.dma_start(
                out=w_in_rows[:].rearrange("p (u e) f -> p u (e f)", u=2),
                in_=w_in.rearrange("(u p e) f -> p u (e f)", u=2, e=2),
            )
            nc.scalar.dma_start(out=scale_bf[:], in_=scale.rearrange("a b (p j) -> (a b p) j", j=4))
            nc.scalar.dma_start(out=bias_bf[:], in_=bias.rearrange("a b (p j) -> (a b p) j", j=4))
            make_identity(nc, identity[:])
            nc.vector.memset(one[:], 1.0)
            nc.scalar.activation(out=unused[:], in_=one[:], func=ACT.Abs_reciprocal_sqrt)
            load_x(0, 2, UNITS)
            for g in range(1, X_TILES):
                load_x(g)

            x_planes[0] = plane_pool.tile([P, 3, UNITS, 256], BF16, name="x_planes", tag="x_planes")
            x_grouped[0] = grouped_pool.tile([P, 3, 4 * GROUP], BF16, name="x_grouped", tag="x_grouped", align_bytes=64)
            rows_0 = x_rows[0][:].rearrange("p u (d m) -> p u d m", m=3)
            half_banks = {}

            def part_half(half):
                units = slice(2 * half, 2 * half + 2)
                for m in range(2):
                    nc.vector.tensor_copy(out=x_planes[0][:, m, units, :], in_=rows_0[:, units, :, m])
                nc.scalar.copy(out=x_planes[0][:, 2, units, :], in_=rows_0[:, units, :, 2])

            def transpose_half(half):
                for bank in range(2):
                    half_banks[bank] = xt_psum.tile([P, UNITS, P], F32, name="x_transposed", tag="x_transposed")
                for m in range(3):
                    for u in range(2):
                        words = x_planes[0][:, m, 2 * half + u, :].bitcast(F32)
                        nc.tensor.transpose(half_banks[m // 2][:, 2 * (m % 2) + u, :], words, identity[:])

            def copy_half(half):
                values = x_grouped[0][:, :, 4 * CHUNK * half : 4 * CHUNK * (half + 1)].bitcast(F32)
                nc.vector.tensor_copy(
                    out=values[:, 0:2, :], in_=half_banks[0][:].rearrange("p (m u) c -> p m (u c)", m=2)
                )
                nc.scalar.copy(out=values[:, 2, :], in_=half_banks[1][:, 0:2, :].rearrange("p u c -> p (u c)"))

            def quantise_half(half, m):
                tokens = tokens_of_chunk(half)
                values = x_grouped[0][:, m, 4 * CHUNK * half : 4 * CHUNK * (half + 1)]
                quantise(x_words[:, m, tokens], x_scales[:, m, tokens], values)

            part_half(0)
            transpose_half(0)
            sorted_rows = w_in_rows[:].rearrange("p j (b a) -> p a b j", a=4)
            sorted_grouped = w_in_grouped[:].rearrange("p (a b) j -> p a b j", a=4)
            copy_half(0)
            nc.gpsimd.tensor_scalar(
                out=sorted_grouped[:, 3, :, :],
                in0=sorted_rows[:, 3, :, :],
                scalar1=1.0,
                scalar2=0.0,
                op0=ALU.mult,
                op1=ALU.add,
            )
            nc.vector.tensor_copy(out=sorted_grouped[:, 0:2, :, :], in_=sorted_rows[:, 0:2, :, :])
            nc.scalar.copy(out=sorted_grouped[:, 2, :, :], in_=sorted_rows[:, 2, :, :])
            quantise_half(0, 0)
            quantise_half(0, 1)
            quantise(w_in_words[:], w_in_scales[:], w_in_grouped[:].rearrange("p c j -> p (c j)"))
            quantise_half(0, 2)
            for m in range(3):
                first_matmul(0, m)
            part_half(1)
            load_x(X_TILES)
            transpose_half(1)
            part_x(1, 0)
            part_x(1, 1)
            square(0, 0)
            copy_half(1)
            for m in range(3):
                quantise_half(1, m)
            square(0, 1)
            square(0, 2)
            for m in range(2):
                transpose_x(1, m)
            for m in range(3):
                first_matmul(1, m)
            copy_x(1, 0)
            part_x(1, 2)
            part_x(2, 0)
            part_x(2, 1)
            copy_x(1, 1)
            nc.scalar.copy(out=scale_f32[:], in_=scale_bf[:])
            nc.scalar.copy(out=bias_f32[:], in_=bias_bf[:])

            def late_work(c):
                if c in (5, 7, 9, 11):
                    clamp((c - 5) // 2, (c - 3) // 2)
                if c == 13:
                    clamp(4, 7)
                if c == 14:
                    clamp(7, 10)
                if c == 15:
                    nc.vector.tensor_copy(out=w_out_grouped[:], in_=w_out_rows[:].rearrange("p j d -> p d j"))
                    clamp(10, 13)
                    quantise(w_out_words[:], w_out_scales[:], w_out_grouped[:].rearrange("p c j -> p (c j)"))
                if c == 17:
                    clamp(13, 16)

            ROOT_SLOT = {14: [], 15: [13, 14], 16: [15]}
            NORM_SLOT = {15: [], 16: [13], 17: [14, 15]}
            for c in range(N_CHUNKS + 2):
                odd = c % 2 == 1
                g = (c + 3) // 2
                if is_chunk(c - 1):
                    sum_squares(c - 1)
                for k in NORM_SLOT.get(c, [c - 2]):
                    if is_chunk(k):
                        norm(k)
                if odd:
                    if is_group(g - 1):
                        quantise_x(g - 1, 2)
                elif is_group(g):
                    quantise_x(g, 0)
                    quantise_x(g, 1)
                if odd and is_group(g):
                    part_x(g, 2)
                if not odd and is_group(g + 1):
                    if c > 0:
                        part_x(g + 1, 0)
                        part_x(g + 1, 1)
                for m in (0, 1) if odd else (2,):
                    if is_group(g):
                        transpose_x(g, m)
                        if by_vector(g, m):
                            copy_x(g, m)
                late_work(c)
                if not odd and is_group(g) and g + X_TILES < N_GROUPS:
                    load_x(g + X_TILES)
                if c == N_CHUNKS - 6:
                    nc.sync.dma_start(out=w_out_rows[:], in_=w_out.rearrange("(p j) d -> p j d", j=4))
                for m in range(3):
                    if 0 < c < N_CHUNKS:
                        square(c, m)
                        if is_chunk(c + 1):
                            first_matmul(c + 1, m)
                for k in ROOT_SLOT.get(c, [c - 1]):
                    if is_chunk(k):
                        inverse_root(k)
                if is_group(g):
                    for m in (0, 1) if odd else (2,):
                        if not by_vector(g, m):
                            copy_x(g, m)
        with ExitStack() as part2:
            g_pool = part2.enter_context(tc.tile_pool(name="g_pool", bufs=3))
            out_pool = part2.enter_context(tc.tile_pool(name="out_pool", bufs=6))
            h_again_psum = part2.enter_context(tc.psum_pool(name="h_again_psum", bufs=4))
            out_psum = part2.enter_context(tc.psum_pool(name="out_psum", bufs=4))

            h_again = {}
            chunk_factors = {}

            def gelu(first, count, j):
                nc.scalar.activation(
                    out=norms[:, j, first : first + count],
                    in_=norms[:, j, first : first + count],
                    func=ACT.Gelu,
                    bias=bias_f32[:, j : j + 1],
                    scale=scale_f32[:, j : j + 1],
                )

            def chunk_factor_tile(c):
                chunk_factors[c] = g_pool.tile(
                    [P, 4, CHUNK], F32, name="chunk_factor", tag="g_or_factor", align_bytes=64
                )
                return chunk_factors[c]

            def tokens_of(values, c):
                return values[:, :, CHUNK * c : CHUNK * (c + 1)]

            def first_matmul_again(c, m):
                tokens = slice(CHUNK * c, CHUNK * (c + 1))
                h_again[(c, m)] = h_again_psum.tile([P, 4, CHUNK], F32, name="h_again", tag="h_again")
                for j in range(4):
                    matmul_mx(
                        h_again[(c, m)][:, j, :],
                        w_in_words[:, hidden(j)],
                        w_in_scales[:, hidden(j)],
                        x_words[:, m, tokens],
                        x_scales[:, m, tokens],
                    )

            for m in range(3):
                first_matmul_again(0, m)
            for first, count in ((0, 128), (128, 128), (256, 256), (512, 512)):
                for j in range(4):
                    gelu(first, count, j)
                if first == 0:
                    nc.vector.tensor_tensor(
                        out=chunk_factor_tile(0)[:], in0=tokens_of(factors, 0), in1=tokens_of(norms, 0), op=ALU.mult
                    )
            later_gelus = [(first, j) for first in range(1024, TOKENS, 256) for j in range(4)]

            for c in range(N_CHUNKS):
                last = c == N_CHUNKS - 1
                if not last:
                    first_matmul_again(c + 1, 0)
                g_grouped = g_pool.tile([P, 3, CHUNK, 4], BF16, name="g_grouped", tag="g_or_factor", align_bytes=64)
                g_words = g_pool.tile([P, 3 * CHUNK], U32, name="g_words", tag="g_words", align_bytes=64)
                g_scales = g_pool.tile([P, 3 * CHUNK], U8, name="g_scales", tag="g_scales", align_bytes=64)
                for m in range(3):
                    nc.vector.tensor_tensor(
                        out=g_grouped[:, m, :, :].rearrange("p (q i) j -> p q j i", i=4),
                        in0=chunk_factors[c][:].rearrange("p j (q i) -> p q j i", i=4),
                        in1=h_again[(c, m)][:].rearrange("p j (q i) -> p q j i", i=4),
                        op=ALU.mult,
                    )
                    if m < 2 and not last:
                        first_matmul_again(c + 1, m + 1)
                if not last:
                    nc.gpsimd.tensor_tensor(
                        out=chunk_factor_tile(c + 1)[:],
                        in0=tokens_of(factors, c + 1),
                        in1=tokens_of(norms, c + 1),
                        op=ALU.mult,
                    )
                quantise(
                    g_words[:, 0 : 2 * CHUNK],
                    g_scales[:, 0 : 2 * CHUNK],
                    g_grouped[:, 0:2, :, :].rearrange("p m t j -> p (m t j)"),
                )
                quantise(
                    g_words[:, 2 * CHUNK : 3 * CHUNK],
                    g_scales[:, 2 * CHUNK : 3 * CHUNK],
                    g_grouped[:, 2, :, :].rearrange("p t j -> p (t j)"),
                )
                out_rows = out_pool.tile([P, ROW], F32, name="out_rows", tag="out_rows")
                for quarter in range(4):
                    channels = slice(P * quarter, P * (quarter + 1))
                    acc = out_psum.tile([P, 3, P], F32, name="acc", tag="acc")
                    for m in range(3):
                        matmul_mx(
                            acc[:, m, :],
                            g_words[:, CHUNK * m : CHUNK * (m + 1)],
                            g_scales[:, CHUNK * m : CHUNK * (m + 1)],
                            w_out_words[:, channels],
                            w_out_scales[:, channels],
                        )
                    interleaved = out_rows[:, 384 * quarter : 384 * (quarter + 1)].rearrange("p (d m) -> p d m", m=3)
                    if last and quarter % 2 == 1:
                        nc.vector.tensor_copy(out=interleaved, in_=acc[:].rearrange("p m d -> p d m"))
                    else:
                        nc.scalar.copy(out=interleaved, in_=acc[:].rearrange("p m d -> p d m"))
                    if last:
                        part = slice(384 * quarter, 384 * (quarter + 1))
                        nc.sync.dma_start(out=out_chunks[:, c, part], in_=out_rows[:, part])
                    elif quarter % 2 == 1:
                        part = slice(384 * (quarter - 1), 384 * (quarter + 1))
                        nc.sync.dma_start(out=out_chunks[:, c, part], in_=out_rows[:, part])
                for first, j in later_gelus[3 * c // 2 : 3 * (c + 1) // 2]:
                    gelu(first, 256, j)
